import numpy as np
import ml_dtypes


def mxq(x, axis, fmt="e4m3"):
    dtype, down = {"e4m3": (ml_dtypes.float8_e4m3fn, 7), "e5m2": (ml_dtypes.float8_e5m2, 14)}[fmt]
    v = np.moveaxis(np.asarray(x, np.float32).astype(ml_dtypes.bfloat16).astype(np.float64), axis, -1)
    blocks = v.reshape(v.shape[:-1] + (-1, 32))
    amax = np.abs(blocks).max(-1, keepdims=True)
    byte = np.maximum(np.where(amax > 0, np.frexp(amax)[1] - 1 + 127, 0) - down, 1)
    scale = np.exp2(byte - 127.0)
    codes = (blocks / scale).astype(np.float32).astype(dtype).astype(np.float64)
    return np.moveaxis((codes * scale).reshape(v.shape), -1, axis)


WIDE = False


def mx_kscale(k):
    if not WIDE:
        return np.ones(k)
    levels = np.array([10, -10, 5, -5, 0])
    if k % 512:
        return np.exp2(np.random.permutation(np.resize(levels, k // 32))).repeat(32)
    a = np.empty((k // 512, 16))
    for p in range(k // 512):
        a[p, :8] = np.random.permutation(np.resize(levels, 8))
        for g in range(8):
            far = levels[np.abs(levels - a[p, g]) >= 10]
            a[p, g + 8] = far[np.random.randint(len(far))]
    return np.exp2(a.ravel()).repeat(32)


BF16 = ml_dtypes.bfloat16


def bf(x):
    return np.asarray(x, np.float32).astype(BF16)


def f64(x):
    return np.asarray(x).astype(np.float64)


B, IN, H, OUT, L, STEPS = 1024, 512, 1024, 128, 3, 3
LN_EPS = 1e-5


def layer_norm(v, g, b):
    m = v.mean(-1, keepdims=True)
    var = ((v - m) ** 2).mean(-1, keepdims=True)
    return (v - m) / np.sqrt(var + LN_EPS) * g + b


def draw0():
    s = mx_kscale(H)
    s = s / s.max()
    return {"h": bf(np.random.standard_normal((B, H)) * s),
            "W_liq": bf(np.random.standard_normal((L, H, H)) / np.sqrt(H) / s),
            "b_liq": bf(np.random.standard_normal((L, H)) * 0.3),
            "g_liq": bf(1.0 + 0.1 * np.random.standard_normal((L, H))),
            "beta_liq": bf(np.random.standard_normal((L, H)) * 0.3)}


def core(h, W_liq, b_liq, g_liq, beta_liq):
    h = f64(h)
    lin = mxq(h, 1, "e4m3") @ mxq(f64(W_liq), 2, "e4m3").transpose(0, 2, 1)
    pre = h[None] + lin + f64(b_liq)[:, None, :]
    return layer_norm(pre, f64(g_liq)[:, None, :], f64(beta_liq)[:, None, :]).sum(0)


def e4m3fn_bytes(y):
    return np.clip(np.asarray(y, np.float64), -448.0, 448.0).astype(np.float32).astype(ml_dtypes.float8_e4m3fn).view(np.uint8)


def e4m3fn_values(b):
    return np.asarray(b, np.uint8).view(ml_dtypes.float8_e4m3fn).astype(np.float64)


def setup_inputs():
    d = draw0()
    x0 = np.asarray(d['W_liq']).astype(np.float64)
    s = (np.max(np.abs(x0), axis=(0, 1), keepdims=True) / 448.0).astype(np.float32)
    out = {}
    for k, v in d.items():
        if k == 'W_liq':
            out['W_liq_bytes'] = e4m3fn_bytes(x0 / s.astype(np.float64))
            out['W_liq_scale'] = s
        else:
            out[k] = v
    return out


def reference(h, W_liq_bytes, W_liq_scale, b_liq, g_liq, beta_liq):
    return core(h, e4m3fn_values(W_liq_bytes) * W_liq_scale.astype(np.float64), b_liq, g_liq, beta_liq)

@@ -1,0 +1,319 @@
+from contextlib import ExitStack
+
+import concourse.mybir as mybir
+from concourse.masks import make_identity
+
+B, H, L = 1024, 1024, 3
+LN_EPS = 1e-5
+FLOPS = 2 * L * B * H * H
+
+F32 = mybir.dt.float32
+BF16 = mybir.dt.bfloat16
+U32 = mybir.dt.uint32
+U8 = mybir.dt.uint8
+FP8 = mybir.dt.float8_e4m3fn
+FP8X4 = mybir.dt.float8_e4m3fn_x4
+ALU = mybir.AluOpType
+ACT = mybir.ActivationFunctionType
+AX = mybir.AxisListType
+
+P = 128
+HALF = 512
+UNITS = 24
+SHIFT_ON_TENSOR = 8
+NORMALISE_ON_VECTOR_FROM = 12
+W_TILES_BEFORE_STEPS = 10
+W_TILES_PER_STEP = (3, 3, 2, 2, 2, 2)
+G0, BETA0, BIAS0 = 0, 32, 64
+
+
+def tile_advancedliquidneuralnetwork_pa_kernel(tc, h, W_liq_bytes, W_liq_scale, b_liq, g_liq, beta_liq, out):
+    nc = tc.nc
+    with ExitStack() as ctx:
+        const = ctx.enter_context(tc.tile_pool(name="const", bufs=1))
+        work = ctx.enter_context(tc.tile_pool(name="work", bufs=2))
+        small = ctx.enter_context(tc.tile_pool(name="small", bufs=8))
+        psum = ctx.enter_context(tc.psum_pool(name="psum", bufs=4))
+
+        scale_all = const.tile([P, H], F32, name="scale_all")
+        nc.scalar.dma_start(out=scale_all[:], in_=W_liq_scale.rearrange("a b k -> (a b k)").partition_broadcast(P))
+        bias_all = const.tile([P, L, H], BF16, name="bias_all")
+        vec_rows = const.tile([P, P], BF16, name="vec_rows")
+        nc.vector.memset(vec_rows[:], 0.0)
+
+        w_view = W_liq_bytes.rearrange("l (c r p) k -> l c p r k", c=2, p=P)
+        h_view = h.rearrange("(i p) k -> i p k", p=P)
+        w_bytes = {}
+        h_rows = []
+
+        def load_w(x):
+            w_bytes[x] = work.tile([P, 4, H], U8, name="w_bytes", tag="w_bytes", bufs=3)
+            nc.sync.dma_start(out=w_bytes[x][:], in_=w_view[x // 2, x % 2])
+
+        def load_h(i):
+            h_rows.append(const.tile([P, H], BF16, name="h_rows%d" % i))
+            nc.sync.dma_start(out=h_rows[i][:], in_=h_view[i])
+
+        load_w(0)
+        load_h(0)
+        load_h(1)
+        load_w(1)
+        load_h(2)
+        load_h(3)
+        nc.scalar.dma_start(out=vec_rows[G0 : G0 + 24, :], in_=g_liq.rearrange("l (j p) -> (l j) p", p=P))
+        nc.scalar.dma_start(out=vec_rows[BETA0 : BETA0 + 24, :], in_=beta_liq.rearrange("l (j p) -> (l j) p", p=P))
+        nc.scalar.dma_start(out=vec_rows[BIAS0 : BIAS0 + 24, :], in_=b_liq.rearrange("l (j p) -> (l j) p", p=P))
+        load_w(2)
+        for i in range(4, 8):
+            load_h(i)
+        nc.sync.dma_start(out=bias_all[:].rearrange("p l n -> p (l n)"), in_=b_liq.rearrange("l n -> (l n)").partition_broadcast(P))
+        for x in range(3, 6):
+            load_w(x)
+
+        one = const.tile([P, 1], F32, name="one")
+        nc.vector.memset(one[:], 1.0)
+        one_root = const.tile([P, 1], F32, name="one_root")
+        nc.scalar.activation(out=one_root[:], in_=one[:], func=ACT.Sqrt)
+        ident_f32 = const.tile([P, P], F32, name="ident_f32")
+        make_identity(nc, ident_f32[:])
+        ident_bf16 = const.tile([P, P], BF16, name="ident_bf16")
+        make_identity(nc, ident_bf16[:])
+
+        lined, h_codes, h_scales, w_codes, w_scales, w_bf16 = {}, {}, {}, {}, {}, {}
+
+        def new_bank(shape, dtype):
+            return psum.tile(shape, dtype, name="bank", tag="bank", bufs=4)
+
+        def turn(rows, dst, r):
+            words = rows.bitcast(F32)
+            bank = new_bank([P, 4, P], F32)
+            for g in range(2):
+                for e in range(2):
+                    nc.tensor.transpose(out=bank[:, 2 * g + e, :], in_=words[:, 256 * g + e : 256 * (g + 1) : 2], identity=ident_f32[:])
+            dst_words = dst[:].rearrange("p g n t -> p (g n t)").bitcast(F32).rearrange("p (g n e) -> p g n e", g=2, e=2)
+            nc.scalar.copy(out=dst_words[:, :, r * P : (r + 1) * P, :], in_=bank[:].rearrange("p (g e) r -> p g r e", e=2))
+
+        def new_lined(key):
+            lined[key] = work.tile([P, 2, HALF, 4], BF16, name="lined", tag="lined", bufs=3, align_bytes=64)
+
+        def quantize(src, codes, scales):
+            for g in range(2):
+                nc.vector.quantize_mx(
+                    out=codes[:, g, :].bitcast(FP8X4),
+                    scales=scales[:, g, :],
+                    in_=src[:, g, :, :].rearrange("p n t -> p (n t)"),
+                )
+
+        def turn_h(i):
+            if i % 4 == 0:
+                new_lined(("h", i // 4))
+            turn(h_rows[i][:], lined[("h", i // 4)], i % 4)
+
+        def quantize_h(bg):
+            h_codes[bg] = const.tile([P, 2, HALF], U32, name="h_codes%d" % bg, align_bytes=64)
+            h_scales[bg] = const.tile([P, 2, HALF], U8, name="h_scales%d" % bg, align_bytes=64)
+            quantize(lined[("h", bg)], h_codes[bg], h_scales[bg])
+
+        def widen(w):
+            w_bf16[w] = work.tile([P, H], BF16, name="w_bf16", tag="w_bf16", bufs=5)
+            nc.vector.tensor_tensor(out=w_bf16[w][:], in0=w_bytes[w // 4][:, w % 4, :].bitcast(FP8), in1=scale_all[:], op=ALU.mult)
+
+        def turn_w(w):
+            if w % 4 == 0:
+                new_lined(("w", w // 4))
+            turn(w_bf16[w][:], lined[("w", w // 4)], w % 4)
+
+        def quantize_w(x):
+            w_codes[x] = const.tile([P, 2, HALF], U32, name="w_codes%d" % x, align_bytes=64)
+            w_scales[x] = const.tile([P, 2, HALF], U8, name="w_scales%d" % x, align_bytes=64)
+            quantize(lined[("w", x)], w_codes[x], w_scales[x])
+
+        shifts, products, pres, row_sums, neg_means, sq_sums, inv_stds, neg_mean_by_std, gained = {}, {}, {}, {}, {}, {}, {}, {}, {}
+
+        def make_shift(n):
+            i, l = 4 * (n // 12) + n % 4, (n % 12) // 4
+            shifts[n] = work.tile([P, H], F32, name="shift", tag="shift", bufs=3)
+            if n < SHIFT_ON_TENSOR:
+                for c in range(2):
+                    bank = new_bank([P, HALF], F32)
+                    for jj in range(4):
+                        col = BIAS0 + 8 * l + 4 * c + jj
+                        nc.tensor.matmul(
+                            out=bank[:, jj * P : (jj + 1) * P],
+                            lhsT=by_feature[:, col : col + 1].to_broadcast([P, P]),
+                            rhs=ident_f32[:],
+                            is_transpose=True,
+                            start=(jj == 0),
+                            stop=False,
+                        )
+                    nc.tensor.matmul(out=bank[:], lhsT=ident_bf16[:], rhs=h_rows[i][:, c * HALF : (c + 1) * HALF], start=False, stop=True)
+                    nc.scalar.copy(out=shifts[n][:, c * HALF : (c + 1) * HALF], in_=bank[:])
+            else:
+                nc.vector.tensor_tensor(out=shifts[n][:], in0=h_rows[i][:], in1=bias_all[:, l, :], op=ALU.add)
+
+        def multiply(n, c):
+            bg, l, u = n // 12, (n % 12) // 4, n % 4
+            products[(n, c)] = psum.tile([P, HALF], F32, name="product", tag="product", bufs=4)
+            for g in range(2):
+                nc.tensor.matmul_mx(
+                    out=products[(n, c)][:],
+                    lhsT=h_codes[bg][:, g, u * P : (u + 1) * P].bitcast(FP8X4),
+                    lhsT_scale=h_scales[bg][:, g, u * P : (u + 1) * P],
+                    rhs=w_codes[2 * l + c][:, g, :].bitcast(FP8X4),
+                    rhs_scale=w_scales[2 * l + c][:, g, :],
+                    start=(g == 0),
+                    stop=(g == 1),
+                )
+
+        def add_shift(n):
+            q, u = n // 4, n % 4
+            if u == 0:
+                row_sums[q] = small.tile([P, 8], F32, name="row_sums")
+            pres[n] = work.tile([P, H], F32, name="pre", tag="pre", bufs=12)
+            for c in range(2):
+                nc.vector.scalar_tensor_tensor(
+                    out=pres[n][:, c * HALF : (c + 1) * HALF],
+                    in0=products[(n, c)][:],
+                    scalar=1.0,
+                    in1=shifts[n][:, c * HALF : (c + 1) * HALF],
+                    op0=ALU.mult,
+                    op1=ALU.add,
+                    accum_out=row_sums[q][:, 2 * u + c : 2 * u + c + 1],
+                )
+
+        def means(q):
+            total = small.tile([P, 4], F32, name="total")
+            neg_means[q] = small.tile([P, 4], F32, name="neg_mean")
+            sq_sums[q] = small.tile([P, 4], F32, name="sq_sum")
+            with tc.high_priority():
+                nc.vector.tensor_reduce(out=total[:], in_=row_sums[q][:].rearrange("p (u c) -> p u c", c=2), axis=AX.X, op=ALU.add)
+                nc.vector.tensor_scalar_mul(out=neg_means[q][:], in0=total[:], scalar1=-1.0 / H)
+
+        def square_sum(n):
+            q, u = n // 4, n % 4
+            squares = work.tile([P, H], BF16, name="squares", tag="squares", bufs=1)
+            nc.scalar.activation(out=squares[:], in_=pres[n][:], func=ACT.Square, bias=neg_means[q][:, u : u + 1], scale=1.0, accum_out=sq_sums[q][:, u : u + 1])
+
+        def inverse_std(q):
+            var_eps = small.tile([P, 4], F32, name="var_eps")
+            std = small.tile([P, 4], F32, name="std")
+            inv_stds[q] = small.tile([P, 4], F32, name="inv_std")
+            neg_mean_by_std[q] = small.tile([P, 4], F32, name="neg_mean_by_std")
+            with tc.high_priority():
+                nc.vector.tensor_scalar(out=var_eps[:], in0=sq_sums[q][:], scalar1=1.0 / H, scalar2=LN_EPS, op0=ALU.mult, op1=ALU.add)
+                nc.scalar.activation(out=std[:], in_=var_eps[:], func=ACT.Sqrt)
+                nc.vector.reciprocal(out=inv_stds[q][:], in_=std[:])
+                nc.vector.tensor_tensor(out=neg_mean_by_std[q][:], in0=neg_means[q][:], in1=inv_stds[q][:], op=ALU.mult)
+
+        def normalise(n):
+            q, u = n // 4, n % 4
+            if n >= NORMALISE_ON_VECTOR_FROM:
+                nc.vector.tensor_scalar(out=pres[n][:], in0=pres[n][:], scalar1=inv_stds[q][:, u : u + 1], scalar2=neg_mean_by_std[q][:, u : u + 1], op0=ALU.mult, op1=ALU.add)
+            else:
+                nc.scalar.activation(out=pres[n][:], in_=pres[n][:], func=ACT.Identity, scale=inv_stds[q][:, u : u + 1], bias=neg_mean_by_std[q][:, u : u + 1])
+
+        def apply_gain(q, j):
+            l, c, jj = q % 3, j // 4, j % 4
+            if l != 1 and jj == 0:
+                gained[(q, c)] = work.tile([P, 4, HALF], F32, name="gained", tag="gained", bufs=6)
+            bank = new_bank([P, HALF], F32)
+            for u in range(4):
+                nc.tensor.transpose(out=bank[:, u * P : (u + 1) * P], in_=pres[4 * q + u][:, j * P : (j + 1) * P], identity=ident_f32[:])
+            gain = by_feature[:, G0 + 8 * l + j : G0 + 8 * l + j + 1]
+            if l == 1:
+                target = gained[(q - 1, c)][:, jj, :]
+                nc.vector.scalar_tensor_tensor(out=target, in0=bank[:], scalar=gain, in1=target, op0=ALU.mult, op1=ALU.add)
+                return
+            beta = beta01[:, j : j + 1] if l == 0 else by_feature[:, BETA0 + 16 + j : BETA0 + 17 + j]
+            if q == UNITS // 4 - 1 and jj == 0:
+                nc.vector.tensor_scalar(out=gained[(q, c)][:, jj, :], in0=bank[:], scalar1=gain, scalar2=beta, op0=ALU.mult, op1=ALU.add)
+            else:
+                nc.scalar.activation(out=gained[(q, c)][:, jj, :], in_=bank[:], func=ACT.Identity, scale=gain, bias=beta)
+
+        def finish(bg, c, u):
+            bank = new_bank([P, HALF], F32)
+            for jj in range(4):
+                for part in range(2):
+                    nc.tensor.matmul(
+                        out=bank[:, jj * P : (jj + 1) * P],
+                        lhsT=gained[(3 * bg + 2 * part, c)][:, jj, u * P : (u + 1) * P],
+                        rhs=ident_f32[:],
+                        is_transpose=True,
+                        start=(part == 0),
+                        stop=(part == 1),
+                    )
+            result = work.tile([P, HALF], F32, name="result", tag="result", bufs=3)
+            nc.scalar.copy(out=result[:], in_=bank[:])
+            r0 = (4 * bg + u) * P
+            nc.sync.dma_start(out=out[r0 : r0 + P, c * HALF : (c + 1) * HALF], in_=result[:])
+
+        table_bank = new_bank([P, P], BF16)
+        nc.tensor.transpose(out=table_bank[:], in_=vec_rows[:], identity=ident_bf16[:])
+        by_feature = const.tile([P, P], F32, name="by_feature")
+        nc.scalar.copy(out=by_feature[:], in_=table_bank[:])
+        beta01 = const.tile([P, 8], F32, name="beta01")
+
+        for w in range(8):
+            turn_h(w)
+            widen(w)
+            turn_w(w)
+            if w == 3:
+                quantize_h(0)
+            if w == 5:
+                quantize_w(0)
+        for w in range(8, W_TILES_BEFORE_STEPS):
+            widen(w)
+        nc.vector.tensor_tensor(out=beta01[:], in0=by_feature[:, BETA0 : BETA0 + 8], in1=by_feature[:, BETA0 + 8 : BETA0 + 16], op=ALU.add)
+        make_shift(0)
+        make_shift(1)
+        quantize_w(1)
+        multiply(0, 0)
+        multiply(0, 1)
+
+        count = {"widened": W_TILES_BEFORE_STEPS, "turned": 8, "quantised": 2, "gains": 0, "finishes": 0}
+        gain_todo = []
+        finish_todo = []
+        for t in range(UNITS + 3):
+            if 4 * (count["quantised"] + 1) <= count["turned"]:
+                quantize_w(count["quantised"])
+                count["quantised"] = count["quantised"] + 1
+            if t == 1:
+                quantize_h(1)
+            if t < UNITS:
+                add_shift(t)
+                if t % 4 == 3:
+                    means(t // 4)
+            if t + 1 < UNITS:
+                multiply(t + 1, 0)
+                multiply(t + 1, 1)
+            for w in range(count["turned"], count["widened"]):
+                turn_w(w)
+            count["turned"] = count["widened"]
+            per_step = 4 if t >= UNITS else 2
+            for i in range(per_step):
+                if count["gains"] < len(gain_todo) and gain_todo[count["gains"]][2] <= t:
+                    q, j = gain_todo[count["gains"]][0], gain_todo[count["gains"]][1]
+                    count["gains"] = count["gains"] + 1
+                    apply_gain(q, j)
+                    if q % 3 == 2 and j % 4 == 3:
+                        finish_todo.extend([(q // 3, j // 4, u, t + 1 if t < UNITS else t) for u in range(4)])
+            for i in range(per_step):
+                if count["finishes"] < len(finish_todo) and finish_todo[count["finishes"]][3] <= t:
+                    bg, c, u = finish_todo[count["finishes"]][0], finish_todo[count["finishes"]][1], finish_todo[count["finishes"]][2]
+                    count["finishes"] = count["finishes"] + 1
+                    finish(bg, c, u)
+            if t + 2 < UNITS:
+                make_shift(t + 2)
+            if t < len(W_TILES_PER_STEP):
+                for w in range(count["widened"], count["widened"] + W_TILES_PER_STEP[t]):
+                    widen(w)
+                count["widened"] = count["widened"] + W_TILES_PER_STEP[t]
+            if t < UNITS and t % 4 == 3:
+                for u in range(4):
+                    square_sum(t - 3 + u)
+            if 4 <= t <= UNITS and t % 4 == 0:
+                inverse_std(t // 4 - 1)
+                for u in range(4):
+                    normalise(t - 4 + u)
+                gain_todo.extend([(t // 4 - 1, j, t + 1 if t < UNITS else t) for j in range(8)])
+        assert count["gains"] == 2 * UNITS and count["finishes"] == 16

@@ -19,12 +19,8 @@ AX = mybir.AxisListType
 
 P = 128
 HALF = 512
-UNITS = 24
-SHIFT_ON_TENSOR = 8
-NORMALISE_ON_VECTOR_FROM = 12
-W_TILES_BEFORE_STEPS = 10
-W_TILES_PER_STEP = (3, 3, 2, 2, 2, 2)
-G0, BETA0, BIAS0 = 0, 32, 64
+QUADS = 6
+PIECES = 3
 
 
 def tile_advancedliquidneuralnetwork_pa_kernel(tc, h, W_liq_bytes, W_liq_scale, b_liq, g_liq, beta_liq, out):
@@ -33,42 +29,44 @@ def tile_advancedliquidneuralnetwork_pa_kernel(tc, h, W_liq_bytes, W_liq_scale, 
         const = ctx.enter_context(tc.tile_pool(name="const", bufs=1))
         work = ctx.enter_context(tc.tile_pool(name="work", bufs=2))
         small = ctx.enter_context(tc.tile_pool(name="small", bufs=8))
-        psum = ctx.enter_context(tc.psum_pool(name="psum", bufs=4))
+        psum = ctx.enter_context(tc.psum_pool(name="psum", bufs=2))
 
         scale_all = const.tile([P, H], F32, name="scale_all")
         nc.scalar.dma_start(out=scale_all[:], in_=W_liq_scale.rearrange("a b k -> (a b k)").partition_broadcast(P))
-        bias_all = const.tile([P, L, H], BF16, name="bias_all")
-        vec_rows = const.tile([P, P], BF16, name="vec_rows")
-        nc.vector.memset(vec_rows[:], 0.0)
 
-        w_view = W_liq_bytes.rearrange("l (c r p) k -> l c p r k", c=2, p=P)
+        w_view = W_liq_bytes.rearrange("l (c m t) k -> l c m t k", c=2, t=4)
         h_view = h.rearrange("(i p) k -> i p k", p=P)
         w_bytes = {}
-        h_rows = []
+        h_rows = {}
 
         def load_w(x):
             w_bytes[x] = work.tile([P, 4, H], U8, name="w_bytes", tag="w_bytes", bufs=3)
             nc.sync.dma_start(out=w_bytes[x][:], in_=w_view[x // 2, x % 2])
 
         def load_h(i):
-            h_rows.append(const.tile([P, H], BF16, name="h_rows%d" % i))
+            h_rows[i] = work.tile([P, H], BF16, name="h_rows", tag="h_rows", bufs=4)
             nc.sync.dma_start(out=h_rows[i][:], in_=h_view[i])
 
         load_w(0)
         load_h(0)
         load_h(1)
-        load_w(1)
         load_h(2)
         load_h(3)
-        nc.scalar.dma_start(out=vec_rows[G0 : G0 + 24, :], in_=g_liq.rearrange("l (j p) -> (l j) p", p=P))
-        nc.scalar.dma_start(out=vec_rows[BETA0 : BETA0 + 24, :], in_=beta_liq.rearrange("l (j p) -> (l j) p", p=P))
-        nc.scalar.dma_start(out=vec_rows[BIAS0 : BIAS0 + 24, :], in_=b_liq.rearrange("l (j p) -> (l j) p", p=P))
-        load_w(2)
+        load_w(1)
+        b_cols_bf16 = const.tile([P, L, 2, 4], BF16, name="b_cols_bf16")
+        nc.scalar.dma_start(out=b_cols_bf16[:], in_=b_liq.rearrange("l (c p t) -> p l c t", c=2, t=4))
+        g_cols_bf16 = const.tile([P, L, 2, 4], BF16, name="g_cols_bf16")
+        nc.scalar.dma_start(out=g_cols_bf16[:], in_=g_liq.rearrange("l (c p t) -> p l c t", c=2, t=4))
         for i in range(4, 8):
             load_h(i)
-        nc.sync.dma_start(out=bias_all[:].rearrange("p l n -> p (l n)"), in_=b_liq.rearrange("l n -> (l n)").partition_broadcast(P))
-        for x in range(3, 6):
+        for x in range(2, 6):
             load_w(x)
+
+        vec_rows = const.tile([P, H], BF16, name="vec_rows")
+        nc.vector.memset(vec_rows[:], 0.0)
+        for s in range(PIECES):
+            nc.gpsimd.dma_start(out=vec_rows[6 * s : 6 * s + 3, :], in_=g_liq)
+            nc.gpsimd.dma_start(out=vec_rows[6 * s + 3 : 6 * s + 6, :], in_=beta_liq)
 
         one = const.tile([P, 1], F32, name="one")
         nc.vector.memset(one[:], 1.0)
@@ -78,23 +76,31 @@ def tile_advancedliquidneuralnetwork_pa_kernel(tc, h, W_liq_bytes, W_liq_scale, 
         make_identity(nc, ident_f32[:])
         ident_bf16 = const.tile([P, P], BF16, name="ident_bf16")
         make_identity(nc, ident_bf16[:])
+        cols = const.tile([P, 2, 8 * L], F32, name="cols")
+        nc.vector.tensor_copy(out=cols[:, 0, :], in_=b_cols_bf16[:].rearrange("p l c t -> p (l c t)"))
+        nc.vector.tensor_copy(out=cols[:, 1, :], in_=g_cols_bf16[:].rearrange("p l c t -> p (l c t)"))
+        stat_rows = {}
+        for bg in range(2):
+            stat_rows[bg] = const.tile([P, 4, P], BF16, name="stat_rows%d" % bg)
+            nc.vector.memset(stat_rows[bg][:], 0.0)
+        vec_perm = const.tile([P, 2, 4, P], BF16, name="vec_perm")
 
         lined, h_codes, h_scales, w_codes, w_scales, w_bf16 = {}, {}, {}, {}, {}, {}
 
-        def new_bank(shape, dtype):
-            return psum.tile(shape, dtype, name="bank", tag="bank", bufs=4)
+        def row_bank(shape, dtype):
+            return psum.tile(shape, dtype, name="row_bank", tag="row_bank", bufs=4)
+
+        def fin_bank(shape, dtype):
+            return psum.tile(shape, dtype, name="fin_bank", tag="fin_bank", bufs=2)
 
         def turn(rows, dst, r):
             words = rows.bitcast(F32)
-            bank = new_bank([P, 4, P], F32)
+            bank = row_bank([P, 4, P], F32)
             for g in range(2):
                 for e in range(2):
                     nc.tensor.transpose(out=bank[:, 2 * g + e, :], in_=words[:, 256 * g + e : 256 * (g + 1) : 2], identity=ident_f32[:])
             dst_words = dst[:].rearrange("p g n t -> p (g n t)").bitcast(F32).rearrange("p (g n e) -> p g n e", g=2, e=2)
             nc.scalar.copy(out=dst_words[:, :, r * P : (r + 1) * P, :], in_=bank[:].rearrange("p (g e) r -> p g r e", e=2))
-
-        def new_lined(key):
-            lined[key] = work.tile([P, 2, HALF, 4], BF16, name="lined", tag="lined", bufs=3, align_bytes=64)
 
         def quantize(src, codes, scales):
             for g in range(2):
@@ -106,7 +112,7 @@ def tile_advancedliquidneuralnetwork_pa_kernel(tc, h, W_liq_bytes, W_liq_scale, 
 
         def turn_h(i):
             if i % 4 == 0:
-                new_lined(("h", i // 4))
+                lined[("h", i // 4)] = const.tile([P, 2, HALF, 4], BF16, name="lined_h%d" % (i // 4), align_bytes=64)
             turn(h_rows[i][:], lined[("h", i // 4)], i % 4)
 
         def quantize_h(bg):
@@ -115,12 +121,12 @@ def tile_advancedliquidneuralnetwork_pa_kernel(tc, h, W_liq_bytes, W_liq_scale, 
             quantize(lined[("h", bg)], h_codes[bg], h_scales[bg])
 
         def widen(w):
-            w_bf16[w] = work.tile([P, H], BF16, name="w_bf16", tag="w_bf16", bufs=5)
+            w_bf16[w] = work.tile([P, H], BF16, name="w_bf16", tag="w_bf16", bufs=4)
             nc.vector.tensor_tensor(out=w_bf16[w][:], in0=w_bytes[w // 4][:, w % 4, :].bitcast(FP8), in1=scale_all[:], op=ALU.mult)
 
         def turn_w(w):
             if w % 4 == 0:
-                new_lined(("w", w // 4))
+                lined[("w", w // 4)] = work.tile([P, 2, HALF, 4], BF16, name="lined", tag="lined", bufs=2, align_bytes=64)
             turn(w_bf16[w][:], lined[("w", w // 4)], w % 4)
 
         def quantize_w(x):
@@ -128,192 +134,192 @@ def tile_advancedliquidneuralnetwork_pa_kernel(tc, h, W_liq_bytes, W_liq_scale, 
             w_scales[x] = const.tile([P, 2, HALF], U8, name="w_scales%d" % x, align_bytes=64)
             quantize(lined[("w", x)], w_codes[x], w_scales[x])
 
-        shifts, products, pres, row_sums, neg_means, sq_sums, inv_stds, neg_mean_by_std, gained = {}, {}, {}, {}, {}, {}, {}, {}, {}
+        products, pre_t, banks, part_sum, neg_mean, sq_sum, rho, spread = {}, {}, {}, {}, {}, {}, {}, {}
+        coef, std0, inv_std0, stat_t = {}, {}, {}, {}
 
-        def make_shift(n):
-            i, l = 4 * (n // 12) + n % 4, (n % 12) // 4
-            shifts[n] = work.tile([P, H], F32, name="shift", tag="shift", bufs=3)
-            if n < SHIFT_ON_TENSOR:
-                for c in range(2):
-                    bank = new_bank([P, HALF], F32)
-                    for jj in range(4):
-                        col = BIAS0 + 8 * l + 4 * c + jj
-                        nc.tensor.matmul(
-                            out=bank[:, jj * P : (jj + 1) * P],
-                            lhsT=by_feature[:, col : col + 1].to_broadcast([P, P]),
-                            rhs=ident_f32[:],
-                            is_transpose=True,
-                            start=(jj == 0),
-                            stop=False,
-                        )
-                    nc.tensor.matmul(out=bank[:], lhsT=ident_bf16[:], rhs=h_rows[i][:, c * HALF : (c + 1) * HALF], start=False, stop=True)
-                    nc.scalar.copy(out=shifts[n][:, c * HALF : (c + 1) * HALF], in_=bank[:])
-            else:
-                nc.vector.tensor_tensor(out=shifts[n][:], in0=h_rows[i][:], in1=bias_all[:, l, :], op=ALU.add)
-
-        def multiply(n, c):
-            bg, l, u = n // 12, (n % 12) // 4, n % 4
-            products[(n, c)] = psum.tile([P, HALF], F32, name="product", tag="product", bufs=4)
+        def multiply(q, j):
+            l, bg, c, t = q // 2, q % 2, j // 4, j % 4
+            products[(q, j)] = psum.tile([P, HALF], F32, name="product", tag="product", bufs=2)
             for g in range(2):
                 nc.tensor.matmul_mx(
-                    out=products[(n, c)][:],
-                    lhsT=h_codes[bg][:, g, u * P : (u + 1) * P].bitcast(FP8X4),
-                    lhsT_scale=h_scales[bg][:, g, u * P : (u + 1) * P],
-                    rhs=w_codes[2 * l + c][:, g, :].bitcast(FP8X4),
-                    rhs_scale=w_scales[2 * l + c][:, g, :],
+                    out=products[(q, j)][:],
+                    lhsT=w_codes[2 * l + c][:, g, t * P : (t + 1) * P].bitcast(FP8X4),
+                    lhsT_scale=w_scales[2 * l + c][:, g, t * P : (t + 1) * P],
+                    rhs=h_codes[bg][:, g, :].bitcast(FP8X4),
+                    rhs_scale=h_scales[bg][:, g, :],
                     start=(g == 0),
                     stop=(g == 1),
                 )
 
-        def add_shift(n):
-            q, u = n // 4, n % 4
-            if u == 0:
-                row_sums[q] = small.tile([P, 8], F32, name="row_sums")
-            pres[n] = work.tile([P, H], F32, name="pre", tag="pre", bufs=12)
+        def add_h(q, j):
+            l, bg, c, t = q // 2, q % 2, j // 4, j % 4
+            if j == 0:
+                pre_t[q] = work.tile([P, 8, HALF], F32, name="pre_t", tag="pre_t", bufs=QUADS)
+            nc.vector.scalar_tensor_tensor(
+                out=pre_t[q][:, j, :],
+                in0=products[(q, j)][:],
+                scalar=cols[:, 0, 8 * l + j : 8 * l + j + 1],
+                in1=lined[("h", bg)][:, c, :, t],
+                op0=ALU.add,
+                op1=ALU.add,
+            )
+
+        def to_rows(q, u):
             for c in range(2):
-                nc.vector.scalar_tensor_tensor(
-                    out=pres[n][:, c * HALF : (c + 1) * HALF],
-                    in0=products[(n, c)][:],
-                    scalar=1.0,
-                    in1=shifts[n][:, c * HALF : (c + 1) * HALF],
-                    op0=ALU.mult,
-                    op1=ALU.add,
-                    accum_out=row_sums[q][:, 2 * u + c : 2 * u + c + 1],
-                )
+                banks[(q, u, c)] = row_bank([P, HALF], F32)
+                for t in range(4):
+                    nc.tensor.transpose(out=banks[(q, u, c)][:, t * P : (t + 1) * P], in_=pre_t[q][:, 4 * c + t, u * P : (u + 1) * P], identity=ident_f32[:])
 
-        def means(q):
+        def stats(q, u):
+            l, bg = q // 2, q % 2
+            if u == 0:
+                part_sum[q] = small.tile([P, 4], F32, name="part_sum")
+                sq_sum[q] = small.tile([P, 8], F32, name="sq_sum")
+                if l == 0:
+                    coef[bg] = const.tile([P, 4, 6], F32, name="coef%d" % bg)
+                else:
+                    neg_mean[q] = small.tile([P, 4], F32, name="neg_mean")
+            mean_col = coef[bg][:, u, 0:1] if l == 0 else neg_mean[q][:, u : u + 1]
+            junk = work.tile([P, HALF], BF16, name="junk", tag="junk", bufs=2)
+            nc.scalar.activation(out=junk[:], in_=banks[(q, u, 0)][:], func=ACT.Copy, scale=-1.0 / (H * HALF), accum_out=part_sum[q][:, u : u + 1])
+            junk = work.tile([P, HALF], BF16, name="junk", tag="junk", bufs=2)
+            nc.scalar.activation(out=junk[:], in_=banks[(q, u, 1)][:], func=ACT.Identity, scale=-1.0 / H, bias=part_sum[q][:, u : u + 1], accum_out=mean_col)
+            for c in range(2):
+                junk = work.tile([P, HALF], BF16, name="junk", tag="junk", bufs=2)
+                nc.scalar.activation(out=junk[:], in_=banks[(q, u, c)][:], func=ACT.Square, bias=mean_col, scale=1.0, accum_out=sq_sum[q][:, 2 * u + c : 2 * u + c + 1])
+
+        def finish_stats(q):
+            l, bg = q // 2, q % 2
             total = small.tile([P, 4], F32, name="total")
-            neg_means[q] = small.tile([P, 4], F32, name="neg_mean")
-            sq_sums[q] = small.tile([P, 4], F32, name="sq_sum")
-            with tc.high_priority():
-                nc.vector.tensor_reduce(out=total[:], in_=row_sums[q][:].rearrange("p (u c) -> p u c", c=2), axis=AX.X, op=ALU.add)
-                nc.vector.tensor_scalar_mul(out=neg_means[q][:], in0=total[:], scalar1=-1.0 / H)
-
-        def square_sum(n):
-            q, u = n // 4, n % 4
-            squares = work.tile([P, H], BF16, name="squares", tag="squares", bufs=1)
-            nc.scalar.activation(out=squares[:], in_=pres[n][:], func=ACT.Square, bias=neg_means[q][:, u : u + 1], scale=1.0, accum_out=sq_sums[q][:, u : u + 1])
-
-        def inverse_std(q):
             var_eps = small.tile([P, 4], F32, name="var_eps")
-            std = small.tile([P, 4], F32, name="std")
-            inv_stds[q] = small.tile([P, 4], F32, name="inv_std")
-            neg_mean_by_std[q] = small.tile([P, 4], F32, name="neg_mean_by_std")
             with tc.high_priority():
-                nc.vector.tensor_scalar(out=var_eps[:], in0=sq_sums[q][:], scalar1=1.0 / H, scalar2=LN_EPS, op0=ALU.mult, op1=ALU.add)
-                nc.scalar.activation(out=std[:], in_=var_eps[:], func=ACT.Sqrt)
-                nc.vector.reciprocal(out=inv_stds[q][:], in_=std[:])
-                nc.vector.tensor_tensor(out=neg_mean_by_std[q][:], in0=neg_means[q][:], in1=inv_stds[q][:], op=ALU.mult)
+                nc.vector.tensor_reduce(out=total[:], in_=sq_sum[q][:].rearrange("p (u c) -> p u c", c=2), axis=AX.X, op=ALU.add)
+                nc.vector.tensor_scalar(out=var_eps[:], in0=total[:], scalar1=1.0 / H, scalar2=LN_EPS, op0=ALU.mult, op1=ALU.add)
+                if l == 0:
+                    std0[bg] = const.tile([P, 4], F32, name="std0_%d" % bg)
+                    inv_std0[bg] = const.tile([P, 4], F32, name="inv_std0_%d" % bg)
+                    nc.scalar.activation(out=std0[bg][:], in_=var_eps[:], func=ACT.Sqrt)
+                    nc.vector.reciprocal(out=inv_std0[bg][:], in_=std0[bg][:])
+                    nc.vector.tensor_copy(out=coef[bg][:, :, 3:6], in_=std0[bg][:].unsqueeze(2).to_broadcast([P, 4, 3]))
+                else:
+                    std = small.tile([P, 4], F32, name="std")
+                    inv_std = small.tile([P, 4], F32, name="inv_std")
+                    rho[q] = small.tile([P, 4], F32, name="rho")
+                    nc.scalar.activation(out=std[:], in_=var_eps[:], func=ACT.Sqrt)
+                    nc.vector.reciprocal(out=inv_std[:], in_=std[:])
+                    nc.vector.tensor_tensor(out=rho[q][:], in0=inv_std[:], in1=std0[bg][:], op=ALU.mult)
+                    nc.vector.tensor_tensor(out=coef[bg][:, :, l], in0=neg_mean[q][:], in1=rho[q][:], op=ALU.mult)
+                    spread[q] = fin_bank([P, HALF], F32)
+                    for u in range(4):
+                        nc.tensor.matmul(
+                            out=spread[q][:, u * P : (u + 1) * P],
+                            lhsT=rho[q][:, u : u + 1].to_broadcast([P, P]),
+                            rhs=ident_f32[:],
+                            is_transpose=True,
+                            start=True,
+                            stop=True,
+                        )
 
-        def normalise(n):
-            q, u = n // 4, n % 4
-            if n >= NORMALISE_ON_VECTOR_FROM:
-                nc.vector.tensor_scalar(out=pres[n][:], in0=pres[n][:], scalar1=inv_stds[q][:, u : u + 1], scalar2=neg_mean_by_std[q][:, u : u + 1], op0=ALU.mult, op1=ALU.add)
-            else:
-                nc.scalar.activation(out=pres[n][:], in_=pres[n][:], func=ACT.Identity, scale=inv_stds[q][:, u : u + 1], bias=neg_mean_by_std[q][:, u : u + 1])
+        def split_coef(bg):
+            rest = coef[bg]
+            with tc.high_priority():
+                for s in range(PIECES):
+                    piece = stat_rows[bg][:, :, 6 * s : 6 * s + 6]
+                    nc.vector.tensor_copy(out=piece, in_=rest[:])
+                    if s + 1 < PIECES:
+                        smaller = small.tile([P, 4, 6], F32, name="smaller")
+                        nc.vector.tensor_tensor(out=smaller[:], in0=rest[:], in1=piece, op=ALU.subtract)
+                        rest = smaller
+                bank = fin_bank([P, 4, P], BF16)
+                for u in range(4):
+                    nc.tensor.transpose(out=bank[:, u, :], in_=stat_rows[bg][:, u, :], identity=ident_bf16[:])
+                stat_t[bg] = const.tile([P, 4, P], BF16, name="stat_t%d" % bg)
+                nc.scalar.copy(out=stat_t[bg][:], in_=bank[:])
 
         def apply_gain(q, j):
-            l, c, jj = q % 3, j // 4, j % 4
-            if l != 1 and jj == 0:
-                gained[(q, c)] = work.tile([P, 4, HALF], F32, name="gained", tag="gained", bufs=6)
-            bank = new_bank([P, HALF], F32)
-            for u in range(4):
-                nc.tensor.transpose(out=bank[:, u * P : (u + 1) * P], in_=pres[4 * q + u][:, j * P : (j + 1) * P], identity=ident_f32[:])
-            gain = by_feature[:, G0 + 8 * l + j : G0 + 8 * l + j + 1]
-            if l == 1:
-                target = gained[(q - 1, c)][:, jj, :]
-                nc.vector.scalar_tensor_tensor(out=target, in0=bank[:], scalar=gain, in1=target, op0=ALU.mult, op1=ALU.add)
-                return
-            beta = beta01[:, j : j + 1] if l == 0 else by_feature[:, BETA0 + 16 + j : BETA0 + 17 + j]
-            if q == UNITS // 4 - 1 and jj == 0:
-                nc.vector.tensor_scalar(out=gained[(q, c)][:, jj, :], in0=bank[:], scalar1=gain, scalar2=beta, op0=ALU.mult, op1=ALU.add)
+            l = q // 2
+            gain = cols[:, 1, 8 * l + j : 8 * l + j + 1]
+            if l == 0:
+                nc.vector.tensor_scalar_mul(out=pre_t[q][:, j, :], in0=pre_t[q][:, j, :], scalar1=gain)
             else:
-                nc.scalar.activation(out=gained[(q, c)][:, jj, :], in_=bank[:], func=ACT.Identity, scale=gain, bias=beta)
+                nc.vector.scalar_tensor_tensor(out=pre_t[q][:, j, :], in0=pre_t[q][:, j, :], scalar=gain, in1=spread[q][:], op0=ALU.mult, op1=ALU.mult)
 
-        def finish(bg, c, u):
-            bank = new_bank([P, HALF], F32)
-            for jj in range(4):
-                for part in range(2):
+        def finish(bg, u, c):
+            bank = fin_bank([P, HALF], F32)
+            for l in range(L):
+                for t in range(4):
                     nc.tensor.matmul(
-                        out=bank[:, jj * P : (jj + 1) * P],
-                        lhsT=gained[(3 * bg + 2 * part, c)][:, jj, u * P : (u + 1) * P],
+                        out=bank[:, t * P : (t + 1) * P],
+                        lhsT=pre_t[2 * l + bg][:, 4 * c + t, u * P : (u + 1) * P],
                         rhs=ident_f32[:],
                         is_transpose=True,
-                        start=(part == 0),
-                        stop=(part == 1),
+                        start=(l == 0 and t == 0),
+                        stop=False,
                     )
+            nc.tensor.matmul(out=bank[:], lhsT=stat_t[bg][:, u, :], rhs=vec_perm[:, c, :, :].rearrange("p t m -> p (t m)"), start=False, stop=True)
             result = work.tile([P, HALF], F32, name="result", tag="result", bufs=3)
-            nc.scalar.copy(out=result[:], in_=bank[:])
+            if u % 2 == 1:
+                nc.vector.tensor_scalar_mul(
+                    out=result[:].rearrange("p (m t) -> p m t", t=4),
+                    in0=bank[:].rearrange("p (t m) -> p m t", t=4),
+                    scalar1=inv_std0[bg][:, u : u + 1],
+                )
+            else:
+                nc.scalar.activation(
+                    out=result[:].rearrange("p (m t) -> p m t", t=4),
+                    in_=bank[:].rearrange("p (t m) -> p m t", t=4),
+                    func=ACT.Copy,
+                    scale=inv_std0[bg][:, u : u + 1],
+                )
             r0 = (4 * bg + u) * P
             nc.sync.dma_start(out=out[r0 : r0 + P, c * HALF : (c + 1) * HALF], in_=result[:])
 
-        table_bank = new_bank([P, P], BF16)
-        nc.tensor.transpose(out=table_bank[:], in_=vec_rows[:], identity=ident_bf16[:])
-        by_feature = const.tile([P, P], F32, name="by_feature")
-        nc.scalar.copy(out=by_feature[:], in_=table_bank[:])
-        beta01 = const.tile([P, 8], F32, name="beta01")
-
-        for w in range(8):
+        for w in range(4):
             turn_h(w)
             widen(w)
             turn_w(w)
-            if w == 3:
-                quantize_h(0)
-            if w == 5:
-                quantize_w(0)
-        for w in range(8, W_TILES_BEFORE_STEPS):
-            widen(w)
-        nc.vector.tensor_tensor(out=beta01[:], in0=by_feature[:, BETA0 : BETA0 + 8], in1=by_feature[:, BETA0 + 8 : BETA0 + 16], op=ALU.add)
-        make_shift(0)
-        make_shift(1)
-        quantize_w(1)
+        quantize_h(0)
+        widen(4)
+        quantize_w(0)
         multiply(0, 0)
-        multiply(0, 1)
 
-        count = {"widened": W_TILES_BEFORE_STEPS, "turned": 8, "quantised": 2, "gains": 0, "finishes": 0}
-        gain_todo = []
-        finish_todo = []
-        for t in range(UNITS + 3):
-            if 4 * (count["quantised"] + 1) <= count["turned"]:
-                quantize_w(count["quantised"])
-                count["quantised"] = count["quantised"] + 1
-            if t == 1:
-                quantize_h(1)
-            if t < UNITS:
-                add_shift(t)
-                if t % 4 == 3:
-                    means(t // 4)
-            if t + 1 < UNITS:
-                multiply(t + 1, 0)
-                multiply(t + 1, 1)
-            for w in range(count["turned"], count["widened"]):
-                turn_w(w)
-            count["turned"] = count["widened"]
-            per_step = 4 if t >= UNITS else 2
-            for i in range(per_step):
-                if count["gains"] < len(gain_todo) and gain_todo[count["gains"]][2] <= t:
-                    q, j = gain_todo[count["gains"]][0], gain_todo[count["gains"]][1]
-                    count["gains"] = count["gains"] + 1
-                    apply_gain(q, j)
-                    if q % 3 == 2 and j % 4 == 3:
-                        finish_todo.extend([(q // 3, j // 4, u, t + 1 if t < UNITS else t) for u in range(4)])
-            for i in range(per_step):
-                if count["finishes"] < len(finish_todo) and finish_todo[count["finishes"]][3] <= t:
-                    bg, c, u = finish_todo[count["finishes"]][0], finish_todo[count["finishes"]][1], finish_todo[count["finishes"]][2]
-                    count["finishes"] = count["finishes"] + 1
-                    finish(bg, c, u)
-            if t + 2 < UNITS:
-                make_shift(t + 2)
-            if t < len(W_TILES_PER_STEP):
-                for w in range(count["widened"], count["widened"] + W_TILES_PER_STEP[t]):
-                    widen(w)
-                count["widened"] = count["widened"] + W_TILES_PER_STEP[t]
-            if t < UNITS and t % 4 == 3:
-                for u in range(4):
-                    square_sum(t - 3 + u)
-            if 4 <= t <= UNITS and t % 4 == 0:
-                inverse_std(t // 4 - 1)
-                for u in range(4):
-                    normalise(t - 4 + u)
-                gain_todo.extend([(t // 4 - 1, j, t + 1 if t < UNITS else t) for j in range(8)])
-        assert count["gains"] == 2 * UNITS and count["finishes"] == 16
+        todo = {}
+
+        def at(step, fn, *args):
+            todo.setdefault(step, []).append((fn, args))
+
+        widen_step = {5: 0, 6: 0, 7: 1}
+        for i in range(8):
+            widen_step[8 + i] = 3 + (3 * i) // 2
+            widen_step[16 + i] = 16 + 2 * i
+        at(0, turn_w, 4)
+        for w in range(5, 24):
+            at(widen_step[w], widen, w)
+            at(widen_step[w] + 1, turn_w, w)
+            if w % 4 == 3:
+                at(widen_step[w] + 2, quantize_w, w // 4)
+        for i in range(4, 8):
+            at(i - 2, turn_h, i)
+        at(6, quantize_h, 1)
+        at(3, nc.scalar.copy, vec_perm[:], vec_rows[:].rearrange("p (c m t) -> p c t m", c=2, t=4))
+        for q in range(QUADS):
+            l, bg, base = q // 2, q % 2, 8 * q
+            for j in range(8):
+                if base + j > 0:
+                    at(base + j - 1, multiply, q, j)
+                at(base + j, add_h, q, j)
+            for u in range(4):
+                at(base + 8 + 2 * u, to_rows, q, u)
+                at(base + 8 + 2 * u, stats, q, u)
+            at(base + 16, finish_stats, q)
+            if l == 2:
+                at(base + 16, split_coef, bg)
+            for j in range(8):
+                at(base + 17 + j, apply_gain, q, j)
+            if l == 2:
+                for c in range(2):
+                    for u in range(4):
+                        at(base + 21 + 4 * c + u, finish, bg, u, c)
+        for step in range(max(todo) + 1):
+            for fn, args in todo.get(step, []):
+                fn(*args)

@@ -21,6 +21,12 @@ P = 128
 HALF = 512
 QUADS = 6
 PIECES = 3
+OPT = {
+    "order": "r", "row": 3, "turn": 2, "product": 2, "spread": 1,
+    "bn": ((1, 3), (3, 3), (3, 2), (5, 3), (5, 2), (5, 1)),
+    "coef_first": False, "fin_tags": (("turn",), ("turn", "product", "row")), "vfinal": (), "merge01": False,
+    "wbf": 4, "lined": 2, "t0": "V", "sum_pe": (), "sum_red": "V", "sum_tag": "spread",
+}
 
 
 def tile_advancedliquidneuralnetwork_pa_kernel(tc, h, W_liq_bytes, W_liq_scale, b_liq, g_liq, beta_liq, out):
@@ -65,8 +71,8 @@ def tile_advancedliquidneuralnetwork_pa_kernel(tc, h, W_liq_bytes, W_liq_scale, 
         vec_rows = const.tile([P, H], BF16, name="vec_rows")
         nc.vector.memset(vec_rows[:], 0.0)
         for s in range(PIECES):
-            nc.gpsimd.dma_start(out=vec_rows[6 * s : 6 * s + 3, :], in_=g_liq)
-            nc.gpsimd.dma_start(out=vec_rows[6 * s + 3 : 6 * s + 6, :], in_=beta_liq)
+            nc.sync.dma_start(out=vec_rows[6 * s : 6 * s + 3, :], in_=g_liq)
+            nc.sync.dma_start(out=vec_rows[6 * s + 3 : 6 * s + 6, :], in_=beta_liq)
 
         one = const.tile([P, 1], F32, name="one")
         nc.vector.memset(one[:], 1.0)
@@ -88,14 +94,20 @@ def tile_advancedliquidneuralnetwork_pa_kernel(tc, h, W_liq_bytes, W_liq_scale, 
         lined, h_codes, h_scales, w_codes, w_scales, w_bf16 = {}, {}, {}, {}, {}, {}
 
         def row_bank(shape, dtype):
-            return psum.tile(shape, dtype, name="row_bank", tag="row_bank", bufs=4)
+            return psum.tile(shape, dtype, name="row_bank", tag="row_bank", bufs=OPT["row"])
 
-        def fin_bank(shape, dtype):
-            return psum.tile(shape, dtype, name="fin_bank", tag="fin_bank", bufs=2)
+        def turn_bank(shape, dtype):
+            return psum.tile(shape, dtype, name="turn_bank", tag="turn_bank", bufs=OPT["turn"])
+
+        def product_bank(shape, dtype):
+            return psum.tile(shape, dtype, name="product", tag="product", bufs=OPT["product"])
+
+        def spread_bank(shape, dtype):
+            return psum.tile(shape, dtype, name="spread_bank", tag="spread_bank", bufs=OPT["spread"])
 
         def turn(rows, dst, r):
             words = rows.bitcast(F32)
-            bank = row_bank([P, 4, P], F32)
+            bank = turn_bank([P, 4, P], F32)
             for g in range(2):
                 for e in range(2):
                     nc.tensor.transpose(out=bank[:, 2 * g + e, :], in_=words[:, 256 * g + e : 256 * (g + 1) : 2], identity=ident_f32[:])
@@ -121,12 +133,12 @@ def tile_advancedliquidneuralnetwork_pa_kernel(tc, h, W_liq_bytes, W_liq_scale, 
             quantize(lined[("h", bg)], h_codes[bg], h_scales[bg])
 
         def widen(w):
-            w_bf16[w] = work.tile([P, H], BF16, name="w_bf16", tag="w_bf16", bufs=4)
+            w_bf16[w] = work.tile([P, H], BF16, name="w_bf16", tag="w_bf16", bufs=OPT["wbf"])
             nc.vector.tensor_tensor(out=w_bf16[w][:], in0=w_bytes[w // 4][:, w % 4, :].bitcast(FP8), in1=scale_all[:], op=ALU.mult)
 
         def turn_w(w):
             if w % 4 == 0:
-                lined[("w", w // 4)] = work.tile([P, 2, HALF, 4], BF16, name="lined", tag="lined", bufs=2, align_bytes=64)
+                lined[("w", w // 4)] = work.tile([P, 2, HALF, 4], BF16, name="lined", tag="lined", bufs=OPT["lined"], align_bytes=64)
             turn(w_bf16[w][:], lined[("w", w // 4)], w % 4)
 
         def quantize_w(x):
@@ -139,7 +151,7 @@ def tile_advancedliquidneuralnetwork_pa_kernel(tc, h, W_liq_bytes, W_liq_scale, 
 
         def multiply(q, j):
             l, bg, c, t = q // 2, q % 2, j // 4, j % 4
-            products[(q, j)] = psum.tile([P, HALF], F32, name="product", tag="product", bufs=2)
+            products[(q, j)] = product_bank([P, HALF], F32)
             for g in range(2):
                 nc.tensor.matmul_mx(
                     out=products[(q, j)][:],
@@ -172,7 +184,7 @@ def tile_advancedliquidneuralnetwork_pa_kernel(tc, h, W_liq_bytes, W_liq_scale, 
 
         def stats(q, u):
             l, bg = q // 2, q % 2
-            if u == 0:
+            if u == 0 and q not in OPT["sum_pe"]:
                 part_sum[q] = small.tile([P, 4], F32, name="part_sum")
                 sq_sum[q] = small.tile([P, 8], F32, name="sq_sum")
                 if l == 0:
@@ -180,10 +192,20 @@ def tile_advancedliquidneuralnetwork_pa_kernel(tc, h, W_liq_bytes, W_liq_scale, 
                 else:
                     neg_mean[q] = small.tile([P, 4], F32, name="neg_mean")
             mean_col = coef[bg][:, u, 0:1] if l == 0 else neg_mean[q][:, u : u + 1]
-            junk = work.tile([P, HALF], BF16, name="junk", tag="junk", bufs=2)
-            nc.scalar.activation(out=junk[:], in_=banks[(q, u, 0)][:], func=ACT.Copy, scale=-1.0 / (H * HALF), accum_out=part_sum[q][:, u : u + 1])
-            junk = work.tile([P, HALF], BF16, name="junk", tag="junk", bufs=2)
-            nc.scalar.activation(out=junk[:], in_=banks[(q, u, 1)][:], func=ACT.Identity, scale=-1.0 / H, bias=part_sum[q][:, u : u + 1], accum_out=mean_col)
+            if (q, u) in OPT["bn"]:
+                bn_st = small.tile([P, 2, 6], F32, name="bn_st")
+                for c in range(2):
+                    nc.vector.bn_stats(out=bn_st[:, c, :], in_=banks[(q, u, c)][:])
+                bn_mv = small.tile([P, 2], F32, name="bn_mv")
+                nc.vector.bn_aggr(out=bn_mv[:], in_=bn_st[:].rearrange("p c s -> p (c s)"))
+                nc.vector.tensor_scalar_mul(out=mean_col, in0=bn_mv[:, 0:1], scalar1=-1.0)
+                nc.vector.tensor_scalar_mul(out=sq_sum[q][:, 2 * u : 2 * u + 2], in0=bn_mv[:, 1:2].to_broadcast([P, 2]), scalar1=H / 2.0)
+                return
+            if q not in OPT["sum_pe"]:
+                junk = work.tile([P, HALF], BF16, name="junk", tag="junk", bufs=2)
+                nc.scalar.activation(out=junk[:], in_=banks[(q, u, 0)][:], func=ACT.Copy, scale=-1.0 / (H * HALF), accum_out=part_sum[q][:, u : u + 1])
+                junk = work.tile([P, HALF], BF16, name="junk", tag="junk", bufs=2)
+                nc.scalar.activation(out=junk[:], in_=banks[(q, u, 1)][:], func=ACT.Identity, scale=-1.0 / H, bias=part_sum[q][:, u : u + 1], accum_out=mean_col)
             for c in range(2):
                 junk = work.tile([P, HALF], BF16, name="junk", tag="junk", bufs=2)
                 nc.scalar.activation(out=junk[:], in_=banks[(q, u, c)][:], func=ACT.Square, bias=mean_col, scale=1.0, accum_out=sq_sum[q][:, 2 * u + c : 2 * u + c + 1])
@@ -209,7 +231,7 @@ def tile_advancedliquidneuralnetwork_pa_kernel(tc, h, W_liq_bytes, W_liq_scale, 
                     nc.vector.reciprocal(out=inv_std[:], in_=std[:])
                     nc.vector.tensor_tensor(out=rho[q][:], in0=inv_std[:], in1=std0[bg][:], op=ALU.mult)
                     nc.vector.tensor_tensor(out=coef[bg][:, :, l], in0=neg_mean[q][:], in1=rho[q][:], op=ALU.mult)
-                    spread[q] = fin_bank([P, HALF], F32)
+                    spread[q] = spread_bank([P, HALF], F32)
                     for u in range(4):
                         nc.tensor.matmul(
                             out=spread[q][:, u * P : (u + 1) * P],
@@ -230,7 +252,7 @@ def tile_advancedliquidneuralnetwork_pa_kernel(tc, h, W_liq_bytes, W_liq_scale, 
                         smaller = small.tile([P, 4, 6], F32, name="smaller")
                         nc.vector.tensor_tensor(out=smaller[:], in0=rest[:], in1=piece, op=ALU.subtract)
                         rest = smaller
-                bank = fin_bank([P, 4, P], BF16)
+                bank = turn_bank([P, 4, P], BF16)
                 for u in range(4):
                     nc.tensor.transpose(out=bank[:, u, :], in_=stat_rows[bg][:, u, :], identity=ident_bf16[:])
                 stat_t[bg] = const.tile([P, 4, P], BF16, name="stat_t%d" % bg)
@@ -239,26 +261,39 @@ def tile_advancedliquidneuralnetwork_pa_kernel(tc, h, W_liq_bytes, W_liq_scale, 
         def apply_gain(q, j):
             l = q // 2
             gain = cols[:, 1, 8 * l + j : 8 * l + j + 1]
-            if l == 0:
+            if l == 0 and OPT["merge01"]:
+                nc.vector.scalar_tensor_tensor(out=pre_t[q + 2][:, j, :], in0=pre_t[q][:, j, :], scalar=gain, in1=pre_t[q + 2][:, j, :], op0=ALU.mult, op1=ALU.add)
+            elif l == 0 and OPT["t0"] == "G":
+                nc.gpsimd.tensor_scalar(out=pre_t[q][:, j, :], in0=pre_t[q][:, j, :], scalar1=gain, scalar2=0.0, op0=ALU.mult, op1=ALU.add)
+            elif l == 0 and OPT["t0"] == "S":
+                nc.scalar.activation(out=pre_t[q][:, j, :], in_=pre_t[q][:, j, :], func=ACT.Copy, scale=gain)
+            elif l == 0:
                 nc.vector.tensor_scalar_mul(out=pre_t[q][:, j, :], in0=pre_t[q][:, j, :], scalar1=gain)
             else:
                 nc.vector.scalar_tensor_tensor(out=pre_t[q][:, j, :], in0=pre_t[q][:, j, :], scalar=gain, in1=spread[q][:], op0=ALU.mult, op1=ALU.mult)
 
         def finish(bg, u, c):
-            bank = fin_bank([P, HALF], F32)
-            for l in range(L):
+            tags = OPT["fin_tags"][bg]
+            tag = tags[(4 * c + u) % len(tags)]
+            bank = {"turn": turn_bank, "product": product_bank, "row": row_bank, "spread": spread_bank}[tag]([P, HALF], F32)
+            first = OPT["coef_first"]
+            if first:
+                nc.tensor.matmul(out=bank[:], lhsT=stat_t[bg][:, u, :], rhs=vec_perm[:, c, :, :].rearrange("p t m -> p (t m)"), start=True, stop=False)
+            ls = [1, 2] if OPT["merge01"] else [0, 1, 2]
+            for l in ls:
                 for t in range(4):
                     nc.tensor.matmul(
                         out=bank[:, t * P : (t + 1) * P],
                         lhsT=pre_t[2 * l + bg][:, 4 * c + t, u * P : (u + 1) * P],
                         rhs=ident_f32[:],
                         is_transpose=True,
-                        start=(l == 0 and t == 0),
-                        stop=False,
+                        start=(not first and l == ls[0] and t == 0),
+                        stop=(first and l == L - 1 and t == 3),
                     )
-            nc.tensor.matmul(out=bank[:], lhsT=stat_t[bg][:, u, :], rhs=vec_perm[:, c, :, :].rearrange("p t m -> p (t m)"), start=False, stop=True)
+            if not first:
+                nc.tensor.matmul(out=bank[:], lhsT=stat_t[bg][:, u, :], rhs=vec_perm[:, c, :, :].rearrange("p t m -> p (t m)"), start=False, stop=True)
             result = work.tile([P, HALF], F32, name="result", tag="result", bufs=3)
-            if u % 2 == 1:
+            if u in OPT["vfinal"]:
                 nc.vector.tensor_scalar_mul(
                     out=result[:].rearrange("p (m t) -> p m t", t=4),
                     in0=bank[:].rearrange("p (t m) -> p m t", t=4),
@@ -274,52 +309,116 @@ def tile_advancedliquidneuralnetwork_pa_kernel(tc, h, W_liq_bytes, W_liq_scale, 
             r0 = (4 * bg + u) * P
             nc.sync.dma_start(out=out[r0 : r0 + P, c * HALF : (c + 1) * HALF], in_=result[:])
 
+        def products_of(q, blocks):
+            for j in blocks:
+                multiply(q, j)
+                add_h(q, j)
+
+        def prepare_w(x):
+            for w in range(4 * x, 4 * x + 4):
+                widen(w)
+                turn_w(w)
+            quantize_w(x)
+
+        def means_by_pe(q):
+            l, bg = q // 2, q % 2
+            part_sum[q] = small.tile([P, 4], F32, name="part_sum")
+            sq_sum[q] = small.tile([P, 8], F32, name="sq_sum")
+            if l == 0:
+                coef[bg] = const.tile([P, 4, 6], F32, name="coef%d" % bg)
+            else:
+                neg_mean[q] = small.tile([P, 4], F32, name="neg_mean")
+            bank = {"turn": turn_bank, "spread": spread_bank, "row": row_bank}[OPT["sum_tag"]]([P, 4, P], F32)
+            for u in range(4):
+                for j in range(8):
+                    nc.tensor.matmul(out=bank[:, u, :], lhsT=pre_t[q][:, j, u * P : (u + 1) * P], rhs=ident_f32[:], is_transpose=True, start=(j == 0), stop=(j == 7))
+            cols4 = coef[bg][:, :, 0] if l == 0 else neg_mean[q][:]
+            if OPT["sum_red"] == "V":
+                nc.vector.tensor_reduce(out=part_sum[q][:], in_=bank[:], axis=AX.X, op=ALU.add)
+                nc.vector.tensor_scalar_mul(out=cols4, in0=part_sum[q][:], scalar1=-1.0 / H)
+            else:
+                for u in range(4):
+                    junk = work.tile([P, HALF], BF16, name="junk", tag="junk", bufs=2)
+                    nc.scalar.activation(out=junk[:, 0:P], in_=bank[:, u, :], func=ACT.Copy, scale=-1.0 / H, accum_out=(coef[bg][:, u, 0:1] if l == 0 else neg_mean[q][:, u : u + 1]))
+
+        def sums_of(q):
+            if q in OPT["sum_pe"]:
+                means_by_pe(q)
+            for u in range(4):
+                to_rows(q, u)
+                stats(q, u)
+            finish_stats(q)
+
+        def gains_of(q):
+            for j in range(8):
+                apply_gain(q, j)
+
+        def last_of(bg):
+            for c in range(2):
+                for t in range(4):
+                    apply_gain(4 + bg, 4 * c + t)
+                for u in range(4):
+                    finish(bg, u, c)
+
+        def perm():
+            nc.scalar.copy(out=vec_perm[:], in_=vec_rows[:].rearrange("p (c m t) -> p c t m", c=2, t=4))
+
         for w in range(4):
             turn_h(w)
             widen(w)
             turn_w(w)
         quantize_h(0)
-        widen(4)
         quantize_w(0)
-        multiply(0, 0)
-
-        todo = {}
-
-        def at(step, fn, *args):
-            todo.setdefault(step, []).append((fn, args))
-
-        widen_step = {5: 0, 6: 0, 7: 1}
-        for i in range(8):
-            widen_step[8 + i] = 3 + (3 * i) // 2
-            widen_step[16 + i] = 16 + 2 * i
-        at(0, turn_w, 4)
-        for w in range(5, 24):
-            at(widen_step[w], widen, w)
-            at(widen_step[w] + 1, turn_w, w)
-            if w % 4 == 3:
-                at(widen_step[w] + 2, quantize_w, w // 4)
+        products_of(0, range(4))
+        prepare_w(1)
+        products_of(0, range(4, 8))
         for i in range(4, 8):
-            at(i - 2, turn_h, i)
-        at(6, quantize_h, 1)
-        at(3, nc.scalar.copy, vec_perm[:], vec_rows[:].rearrange("p (c m t) -> p c t m", c=2, t=4))
-        for q in range(QUADS):
-            l, bg, base = q // 2, q % 2, 8 * q
-            for j in range(8):
-                if base + j > 0:
-                    at(base + j - 1, multiply, q, j)
-                at(base + j, add_h, q, j)
-            for u in range(4):
-                at(base + 8 + 2 * u, to_rows, q, u)
-                at(base + 8 + 2 * u, stats, q, u)
-            at(base + 16, finish_stats, q)
-            if l == 2:
-                at(base + 16, split_coef, bg)
-            for j in range(8):
-                at(base + 17 + j, apply_gain, q, j)
-            if l == 2:
-                for c in range(2):
-                    for u in range(4):
-                        at(base + 21 + 4 * c + u, finish, bg, u, c)
-        for step in range(max(todo) + 1):
-            for fn, args in todo.get(step, []):
-                fn(*args)
+            turn_h(i)
+        quantize_h(1)
+        if OPT["order"] == "l":
+            products_of(1, range(8))
+            perm()
+            for l in range(L):
+                if l > 0:
+                    products_of(2 * l, range(8))
+                    products_of(2 * l + 1, range(8))
+                if l + 1 < L:
+                    prepare_w(2 * l + 2)
+                    prepare_w(2 * l + 3)
+                for bg in range(2):
+                    sums_of(2 * l + bg)
+                    if l == L - 1:
+                        split_coef(bg)
+            if OPT["merge01"]:
+                for q in (2, 3, 0, 1):
+                    gains_of(q)
+            else:
+                for q in range(4):
+                    gains_of(q)
+            for bg in range(2):
+                last_of(bg)
+        elif OPT["order"] == "r":
+            perm()
+            prepare_w(2)
+            prepare_w(3)
+            sums_of(0)
+            products_of(2, range(8))
+            prepare_w(4)
+            prepare_w(5)
+            sums_of(2)
+            products_of(4, range(8))
+            sums_of(4)
+            split_coef(0)
+            products_of(1, range(8))
+            sums_of(1)
+            products_of(3, range(8))
+            sums_of(3)
+            products_of(5, range(8))
+            for q in ((2, 0) if OPT["merge01"] else (0, 2)):
+                gains_of(q)
+            last_of(0)
+            sums_of(5)
+            split_coef(1)
+            for q in ((3, 1) if OPT["merge01"] else (1, 3)):
+                gains_of(q)
+            last_of(1)

@@ -23,7 +23,7 @@ QUADS = 6
 PIECES = 3
 OPT = {
     "order": "r", "row": 3, "turn": 2, "product": 2, "spread": 1,
-    "bn": ((1, 3), (3, 3), (3, 2), (5, 3), (5, 2), (5, 1)),
+    "bn": ((1, 3), (3, 3), (3, 2), (5, 3), (5, 2), (5, 1)), "bnq": (), "t0g": (), "t0s": (), "vfinal1": (1, 3),
     "coef_first": False, "fin_tags": (("turn",), ("turn", "product", "row")), "vfinal": (), "merge01": False,
     "wbf": 4, "lined": 2, "t0": "V", "sum_pe": (), "sum_red": "V", "sum_tag": "spread",
 }
@@ -47,7 +47,11 @@ def tile_advancedliquidneuralnetwork_pa_kernel(tc, h, W_liq_bytes, W_liq_scale, 
 
         def load_w(x):
             w_bytes[x] = work.tile([P, 4, H], U8, name="w_bytes", tag="w_bytes", bufs=3)
-            nc.sync.dma_start(out=w_bytes[x][:], in_=w_view[x // 2, x % 2])
+            if x == 0:
+                for t in range(4):
+                    nc.sync.dma_start(out=w_bytes[x][:, t, :], in_=w_view[0, 0, :, t, :])
+            else:
+                nc.sync.dma_start(out=w_bytes[x][:], in_=w_view[x // 2, x % 2])
 
         def load_h(i):
             h_rows[i] = work.tile([P, H], BF16, name="h_rows", tag="h_rows", bufs=4)
@@ -147,7 +151,7 @@ def tile_advancedliquidneuralnetwork_pa_kernel(tc, h, W_liq_bytes, W_liq_scale, 
             quantize(lined[("w", x)], w_codes[x], w_scales[x])
 
         products, pre_t, banks, part_sum, neg_mean, sq_sum, rho, spread = {}, {}, {}, {}, {}, {}, {}, {}
-        coef, std0, inv_std0, stat_t = {}, {}, {}, {}
+        coef, std0, inv_std0, stat_t, bn_all = {}, {}, {}, {}, {}
 
         def multiply(q, j):
             l, bg, c, t = q // 2, q % 2, j // 4, j % 4
@@ -192,6 +196,14 @@ def tile_advancedliquidneuralnetwork_pa_kernel(tc, h, W_liq_bytes, W_liq_scale, 
                 else:
                     neg_mean[q] = small.tile([P, 4], F32, name="neg_mean")
             mean_col = coef[bg][:, u, 0:1] if l == 0 else neg_mean[q][:, u : u + 1]
+            if q in OPT["bnq"]:
+                if u == 0:
+                    bn_all[q] = small.tile([P, 4, 2], F32, name="bn_all")
+                bn_st = small.tile([P, 2, 6], F32, name="bn_st")
+                for c in range(2):
+                    nc.vector.bn_stats(out=bn_st[:, c, :], in_=banks[(q, u, c)][:])
+                nc.vector.bn_aggr(out=bn_all[q][:, u, :], in_=bn_st[:].rearrange("p c s -> p (c s)"))
+                return
             if (q, u) in OPT["bn"]:
                 bn_st = small.tile([P, 2, 6], F32, name="bn_st")
                 for c in range(2):
@@ -215,8 +227,12 @@ def tile_advancedliquidneuralnetwork_pa_kernel(tc, h, W_liq_bytes, W_liq_scale, 
             total = small.tile([P, 4], F32, name="total")
             var_eps = small.tile([P, 4], F32, name="var_eps")
             with tc.high_priority():
-                nc.vector.tensor_reduce(out=total[:], in_=sq_sum[q][:].rearrange("p (u c) -> p u c", c=2), axis=AX.X, op=ALU.add)
-                nc.vector.tensor_scalar(out=var_eps[:], in0=total[:], scalar1=1.0 / H, scalar2=LN_EPS, op0=ALU.mult, op1=ALU.add)
+                if q in OPT["bnq"]:
+                    nc.vector.tensor_scalar_add(out=var_eps[:], in0=bn_all[q][:, :, 1], scalar1=LN_EPS)
+                    nc.vector.tensor_scalar_mul(out=(coef[bg][:, :, 0] if l == 0 else neg_mean[q][:]), in0=bn_all[q][:, :, 0], scalar1=-1.0)
+                else:
+                    nc.vector.tensor_reduce(out=total[:], in_=sq_sum[q][:].rearrange("p (u c) -> p u c", c=2), axis=AX.X, op=ALU.add)
+                    nc.vector.tensor_scalar(out=var_eps[:], in0=total[:], scalar1=1.0 / H, scalar2=LN_EPS, op0=ALU.mult, op1=ALU.add)
                 if l == 0:
                     std0[bg] = const.tile([P, 4], F32, name="std0_%d" % bg)
                     inv_std0[bg] = const.tile([P, 4], F32, name="inv_std0_%d" % bg)
@@ -263,9 +279,9 @@ def tile_advancedliquidneuralnetwork_pa_kernel(tc, h, W_liq_bytes, W_liq_scale, 
             gain = cols[:, 1, 8 * l + j : 8 * l + j + 1]
             if l == 0 and OPT["merge01"]:
                 nc.vector.scalar_tensor_tensor(out=pre_t[q + 2][:, j, :], in0=pre_t[q][:, j, :], scalar=gain, in1=pre_t[q + 2][:, j, :], op0=ALU.mult, op1=ALU.add)
-            elif l == 0 and OPT["t0"] == "G":
+            elif l == 0 and q in OPT["t0g"]:
                 nc.gpsimd.tensor_scalar(out=pre_t[q][:, j, :], in0=pre_t[q][:, j, :], scalar1=gain, scalar2=0.0, op0=ALU.mult, op1=ALU.add)
-            elif l == 0 and OPT["t0"] == "S":
+            elif l == 0 and q in OPT["t0s"]:
                 nc.scalar.activation(out=pre_t[q][:, j, :], in_=pre_t[q][:, j, :], func=ACT.Copy, scale=gain)
             elif l == 0:
                 nc.vector.tensor_scalar_mul(out=pre_t[q][:, j, :], in0=pre_t[q][:, j, :], scalar1=gain)
@@ -292,8 +308,11 @@ def tile_advancedliquidneuralnetwork_pa_kernel(tc, h, W_liq_bytes, W_liq_scale, 
                     )
             if not first:
                 nc.tensor.matmul(out=bank[:], lhsT=stat_t[bg][:, u, :], rhs=vec_perm[:, c, :, :].rearrange("p t m -> p (t m)"), start=False, stop=True)
-            result = work.tile([P, HALF], F32, name="result", tag="result", bufs=3)
-            if u in OPT["vfinal"]:
+            if (4 * c + u) % 2 == 0:
+                result = work.tile([P, HALF], F32, name="h_rows", tag="h_rows", bufs=4)
+            else:
+                result = work.tile([P, HALF], F32, name="w_bf16", tag="w_bf16", bufs=OPT["wbf"])
+            if u in (OPT["vfinal1"] if bg == 1 else OPT["vfinal"]):
                 nc.vector.tensor_scalar_mul(
                     out=result[:].rearrange("p (m t) -> p m t", t=4),
                     in0=bank[:].rearrange("p (t m) -> p m t", t=4),

@@ -24,7 +24,7 @@ PIECES = 3
 OPT = {
     "order": "r", "row": 3, "turn": 2, "product": 2, "spread": 1,
     "bn": ((1, 3), (3, 3), (3, 2), (5, 3), (5, 2), (5, 1)), "bnq": (), "t0g": (), "t0s": (), "vfinal1": (1, 3),
-    "coef_first": False, "fin_tags": (("turn",), ("turn", "product", "row")), "vfinal": (), "merge01": False,
+    "coef_first": False, "fin_tags": (("turn",), ("turn", "product", "row")), "vfinal": (), "merge01": True,
     "wbf": 4, "lined": 2, "t0": "V", "sum_pe": (), "sum_red": "V", "sum_tag": "spread",
 }
 

@@ -47,26 +47,21 @@ def tile_advancedliquidneuralnetwork_pa_kernel(tc, h, W_liq_bytes, W_liq_scale, 
 
         def load_w(x):
             w_bytes[x] = work.tile([P, 4, H], U8, name="w_bytes", tag="w_bytes", bufs=3)
-            if x == 0:
-                for t in range(4):
-                    nc.sync.dma_start(out=w_bytes[x][:, t, :], in_=w_view[0, 0, :, t, :])
-            else:
-                nc.sync.dma_start(out=w_bytes[x][:], in_=w_view[x // 2, x % 2])
+            nc.sync.dma_start(out=w_bytes[x][:], in_=w_view[x // 2, x % 2])
 
         def load_h(i):
             h_rows[i] = work.tile([P, H], BF16, name="h_rows", tag="h_rows", bufs=4)
             nc.sync.dma_start(out=h_rows[i][:], in_=h_view[i])
 
-        load_w(0)
-        load_h(0)
-        load_h(1)
-        load_h(2)
-        load_h(3)
+        w_bytes[0] = work.tile([P, 4, H], U8, name="w_bytes", tag="w_bytes", bufs=3)
+        for t in range(4):
+            nc.sync.dma_start(out=w_bytes[0][:, t, :], in_=w_view[0, 0, :, t, :])
+            load_h(t)
         load_w(1)
         b_cols_bf16 = const.tile([P, L, 2, 4], BF16, name="b_cols_bf16")
-        nc.scalar.dma_start(out=b_cols_bf16[:], in_=b_liq.rearrange("l (c p t) -> p l c t", c=2, t=4))
+        nc.sync.dma_start(out=b_cols_bf16[:], in_=b_liq.rearrange("l (c p t) -> p l c t", c=2, t=4))
         g_cols_bf16 = const.tile([P, L, 2, 4], BF16, name="g_cols_bf16")
-        nc.scalar.dma_start(out=g_cols_bf16[:], in_=g_liq.rearrange("l (c p t) -> p l c t", c=2, t=4))
+        nc.sync.dma_start(out=g_cols_bf16[:], in_=g_liq.rearrange("l (c p t) -> p l c t", c=2, t=4))
         for i in range(4, 8):
             load_h(i)
         for x in range(2, 6):

@@ -5,7 +5,6 @@ from concourse.masks import make_identity
 
 B, H, L = 1024, 1024, 3
 LN_EPS = 1e-5
-FLOPS = 2 * L * B * H * H
 
 F32 = mybir.dt.float32
 BF16 = mybir.dt.bfloat16
@@ -15,18 +14,17 @@ FP8 = mybir.dt.float8_e4m3fn
 FP8X4 = mybir.dt.float8_e4m3fn_x4
 ALU = mybir.AluOpType
 ACT = mybir.ActivationFunctionType
-AX = mybir.AxisListType
 
 P = 128
 HALF = 512
-QUADS = 6
+GROUPS = 2
+TILES = 4
+BLOCKS = 8
+QUADS = GROUPS * L
 PIECES = 3
-OPT = {
-    "order": "r", "row": 3, "turn": 2, "product": 2, "spread": 1,
-    "bn": ((1, 3), (3, 3), (3, 2), (5, 3), (5, 2), (5, 1)), "bnq": (), "t0g": (), "t0s": (), "vfinal1": (1, 3),
-    "coef_first": False, "fin_tags": (("turn",), ("turn", "product", "row")), "vfinal": (), "merge01": True,
-    "wbf": 4, "lined": 2, "t0": "V", "sum_pe": (), "sum_red": "V", "sum_tag": "spread",
-}
+BANKS = {"product": 2, "turn": 2, "row": 4}
+LEAD = 3
+VECTOR_SUMS = ((1, 3), (3, 3))
 
 
 def tile_advancedliquidneuralnetwork_pa_kernel(tc, h, W_liq_bytes, W_liq_scale, b_liq, g_liq, beta_liq, out):
@@ -37,127 +35,145 @@ def tile_advancedliquidneuralnetwork_pa_kernel(tc, h, W_liq_bytes, W_liq_scale, 
         small = ctx.enter_context(tc.tile_pool(name="small", bufs=8))
         psum = ctx.enter_context(tc.psum_pool(name="psum", bufs=2))
 
-        scale_all = const.tile([P, H], F32, name="scale_all")
-        nc.scalar.dma_start(out=scale_all[:], in_=W_liq_scale.rearrange("a b k -> (a b k)").partition_broadcast(P))
+        scale_cols = const.tile([P, 2, 4], F32, name="scale_cols")
+        nc.scalar.dma_start(out=scale_cols[:], in_=W_liq_scale.rearrange("a b (c p m) -> (a b p) c m", c=2, m=4))
 
         w_view = W_liq_bytes.rearrange("l (c m t) k -> l c m t k", c=2, t=4)
         h_view = h.rearrange("(i p) k -> i p k", p=P)
-        w_bytes = {}
-        h_rows = {}
+        w_bytes, h_rows = {}, {}
 
         def load_w(x):
             w_bytes[x] = work.tile([P, 4, H], U8, name="w_bytes", tag="w_bytes", bufs=3)
-            nc.sync.dma_start(out=w_bytes[x][:], in_=w_view[x // 2, x % 2])
+            if x == 0:
+                for t in range(4):
+                    nc.sync.dma_start(out=w_bytes[x][:, t, :], in_=w_view[0, 0, :, t, :])
+                    load_h(t)
+            else:
+                nc.sync.dma_start(out=w_bytes[x][:], in_=w_view[x // 2, x % 2])
 
         def load_h(i):
             h_rows[i] = work.tile([P, H], BF16, name="h_rows", tag="h_rows", bufs=4)
             nc.sync.dma_start(out=h_rows[i][:], in_=h_view[i])
 
-        w_bytes[0] = work.tile([P, 4, H], U8, name="w_bytes", tag="w_bytes", bufs=3)
-        for t in range(4):
-            nc.sync.dma_start(out=w_bytes[0][:, t, :], in_=w_view[0, 0, :, t, :])
-            load_h(t)
+        load_w(0)
         load_w(1)
-        b_cols_bf16 = const.tile([P, L, 2, 4], BF16, name="b_cols_bf16")
-        nc.sync.dma_start(out=b_cols_bf16[:], in_=b_liq.rearrange("l (c p t) -> p l c t", c=2, t=4))
-        g_cols_bf16 = const.tile([P, L, 2, 4], BF16, name="g_cols_bf16")
-        nc.sync.dma_start(out=g_cols_bf16[:], in_=g_liq.rearrange("l (c p t) -> p l c t", c=2, t=4))
+        b_cols = const.tile([P, L, 2, 4], BF16, name="b_cols")
+        nc.sync.dma_start(out=b_cols[:], in_=b_liq.rearrange("l (c p t) -> p l c t", c=2, t=4))
         for i in range(4, 8):
             load_h(i)
-        for x in range(2, 6):
-            load_w(x)
-
+        load_w(2)
+        g_cols = const.tile([P, L, 2, 4], BF16, name="g_cols")
+        nc.sync.dma_start(out=g_cols[:], in_=g_liq.rearrange("l (c p t) -> p l c t", c=2, t=4))
         vec_rows = const.tile([P, H], BF16, name="vec_rows")
         nc.vector.memset(vec_rows[:], 0.0)
         for s in range(PIECES):
             nc.sync.dma_start(out=vec_rows[6 * s : 6 * s + 3, :], in_=g_liq)
             nc.sync.dma_start(out=vec_rows[6 * s + 3 : 6 * s + 6, :], in_=beta_liq)
+        for x in range(3, 6):
+            load_w(x)
 
         one = const.tile([P, 1], F32, name="one")
         nc.vector.memset(one[:], 1.0)
+        eps_col = const.tile([P, 1], F32, name="eps_col")
+        nc.vector.tensor_scalar_mul(out=eps_col[:], in0=one[:], scalar1=LN_EPS)
         one_root = const.tile([P, 1], F32, name="one_root")
         nc.scalar.activation(out=one_root[:], in_=one[:], func=ACT.Sqrt)
         ident_f32 = const.tile([P, P], F32, name="ident_f32")
         make_identity(nc, ident_f32[:])
         ident_bf16 = const.tile([P, P], BF16, name="ident_bf16")
         make_identity(nc, ident_bf16[:])
-        cols = const.tile([P, 2, 8 * L], F32, name="cols")
-        nc.vector.tensor_copy(out=cols[:, 0, :], in_=b_cols_bf16[:].rearrange("p l c t -> p (l c t)"))
-        nc.vector.tensor_copy(out=cols[:, 1, :], in_=g_cols_bf16[:].rearrange("p l c t -> p (l c t)"))
-        stat_rows = {}
-        for bg in range(2):
-            stat_rows[bg] = const.tile([P, 4, P], BF16, name="stat_rows%d" % bg)
-            nc.vector.memset(stat_rows[bg][:], 0.0)
+        coef_rows = {}
+        for bg in range(GROUPS):
+            coef_rows[bg] = const.tile([P, TILES, P], BF16, name="coef_rows%d" % bg)
+            nc.vector.memset(coef_rows[bg][:], 0.0)
+        scale_all = const.tile([P, H], F32, name="scale_all")
         vec_perm = const.tile([P, 2, 4, P], BF16, name="vec_perm")
 
-        lined, h_codes, h_scales, w_codes, w_scales, w_bf16 = {}, {}, {}, {}, {}, {}
+        def bank_of(tag, dtype=F32):
+            return psum.tile([P, 4, P], dtype, name=tag, tag=tag, bufs=BANKS[tag])
 
-        def row_bank(shape, dtype):
-            return psum.tile(shape, dtype, name="row_bank", tag="row_bank", bufs=OPT["row"])
+        def flat(bank):
+            return bank[:].rearrange("p a b -> p (a b)")
 
-        def turn_bank(shape, dtype):
-            return psum.tile(shape, dtype, name="turn_bank", tag="turn_bank", bufs=OPT["turn"])
+        def spread_scales():
+            for c in range(2):
+                bank = bank_of("product")
+                for m in range(4):
+                    turn(bank[:, m, :], scale_cols[:, c, m : m + 1].to_broadcast([P, P]))
+                half = scale_all[:, c * HALF : (c + 1) * HALF].rearrange("q (p m) -> q p m", m=4)
+                if c == 0:
+                    nc.vector.tensor_copy(out=half, in_=bank[:].rearrange("q m p -> q p m"))
+                else:
+                    nc.scalar.copy(out=half, in_=bank[:].rearrange("q m p -> q p m"))
 
-        def product_bank(shape, dtype):
-            return psum.tile(shape, dtype, name="product", tag="product", bufs=OPT["product"])
+        def order_vectors():
+            nc.scalar.copy(out=vec_perm[:], in_=vec_rows[:].rearrange("p (c m t) -> p c t m", c=2, t=4))
 
-        def spread_bank(shape, dtype):
-            return psum.tile(shape, dtype, name="spread_bank", tag="spread_bank", bufs=OPT["spread"])
+        def turn(bank, block, start=True, stop=True):
+            nc.tensor.matmul(out=bank, lhsT=block, rhs=ident_f32[:], is_transpose=True, start=start, stop=stop)
 
-        def turn(rows, dst, r):
+        turned, lined, codes, scales, w_bf16 = {}, {}, {}, {}, {}
+
+        def turn_words(key, rows, tag):
             words = rows.bitcast(F32)
-            bank = turn_bank([P, 4, P], F32)
+            turned[key] = bank_of(tag)
             for g in range(2):
                 for e in range(2):
-                    nc.tensor.transpose(out=bank[:, 2 * g + e, :], in_=words[:, 256 * g + e : 256 * (g + 1) : 2], identity=ident_f32[:])
-            dst_words = dst[:].rearrange("p g n t -> p (g n t)").bitcast(F32).rearrange("p (g n e) -> p g n e", g=2, e=2)
-            nc.scalar.copy(out=dst_words[:, :, r * P : (r + 1) * P, :], in_=bank[:].rearrange("p (g e) r -> p g r e", e=2))
+                    turn(turned[key][:, 2 * g + e, :], words[:, 256 * g + e : 256 * (g + 1) : 2])
 
-        def quantize(src, codes, scales):
-            for g in range(2):
-                nc.vector.quantize_mx(
-                    out=codes[:, g, :].bitcast(FP8X4),
-                    scales=scales[:, g, :],
-                    in_=src[:, g, :, :].rearrange("p n t -> p (n t)"),
-                )
+        def line_up(key, dst, first_row):
+            words = dst[:].rearrange("p g r t -> p (g r t)").bitcast(F32).rearrange("p (g r e) -> p g r e", g=2, e=2)
+            nc.scalar.copy(out=words[:, :, first_row : first_row + P, :], in_=turned[key][:].rearrange("p (g e) r -> p g r e", e=2))
+
+        def quantize(key, rows):
+            name = "%s%d" % key
+            codes[key] = const.tile([P, 2, rows], U32, name="codes_" + name, align_bytes=64)
+            scales[key] = const.tile([P, 2, rows], U8, name="scales_" + name, align_bytes=64)
+            nc.vector.quantize_mx(
+                out=codes[key][:].rearrange("p g r -> p (g r)").bitcast(FP8X4),
+                scales=scales[key][:].rearrange("p g r -> p (g r)"),
+                in_=lined[key][:].rearrange("p g r t -> p (g r t)"),
+            )
 
         def turn_h(i):
-            if i % 4 == 0:
-                lined[("h", i // 4)] = const.tile([P, 2, HALF, 4], BF16, name="lined_h%d" % (i // 4), align_bytes=64)
-            turn(h_rows[i][:], lined[("h", i // 4)], i % 4)
+            turn_words(("row tile", i), h_rows[i][:], "turn")
+
+        def line_h(i):
+            key = ("h", i // TILES)
+            if i % TILES == 0:
+                lined[key] = const.tile([P, 2, HALF, 4], BF16, name="lined_h%d" % key[1], align_bytes=64)
+            line_up(("row tile", i), lined[key], i % TILES * P)
 
         def quantize_h(bg):
-            h_codes[bg] = const.tile([P, 2, HALF], U32, name="h_codes%d" % bg, align_bytes=64)
-            h_scales[bg] = const.tile([P, 2, HALF], U8, name="h_scales%d" % bg, align_bytes=64)
-            quantize(lined[("h", bg)], h_codes[bg], h_scales[bg])
+            quantize(("h", bg), HALF)
 
         def widen(w):
-            w_bf16[w] = work.tile([P, H], BF16, name="w_bf16", tag="w_bf16", bufs=OPT["wbf"])
-            nc.vector.tensor_tensor(out=w_bf16[w][:], in0=w_bytes[w // 4][:, w % 4, :].bitcast(FP8), in1=scale_all[:], op=ALU.mult)
+            w_bf16[w] = work.tile([P, H], BF16, name="w_bf16", tag="w_bf16", bufs=4)
+            for part in (slice(0, HALF), slice(HALF, H)) if w == 0 else (slice(0, H),):
+                nc.vector.tensor_tensor(out=w_bf16[w][:, part], in0=w_bytes[w // 4][:, w % 4, part].bitcast(FP8), in1=scale_all[:, part], op=ALU.mult)
 
-        def turn_w(w):
-            if w % 4 == 0:
-                lined[("w", w // 4)] = work.tile([P, 2, HALF, 4], BF16, name="lined", tag="lined", bufs=OPT["lined"], align_bytes=64)
-            turn(w_bf16[w][:], lined[("w", w // 4)], w % 4)
+        def turn_w(w, tag):
+            turn_words(("w", w), w_bf16[w][:], tag)
 
-        def quantize_w(x):
-            w_codes[x] = const.tile([P, 2, HALF], U32, name="w_codes%d" % x, align_bytes=64)
-            w_scales[x] = const.tile([P, 2, HALF], U8, name="w_scales%d" % x, align_bytes=64)
-            quantize(lined[("w", x)], w_codes[x], w_scales[x])
+        def line_w(w):
+            lined[("w", w)] = work.tile([P, 2, P, 4], BF16, name="lined_w", tag="lined_w", bufs=8, align_bytes=64)
+            line_up(("w", w), lined[("w", w)], 0)
 
-        products, pre_t, banks, part_sum, neg_mean, sq_sum, rho, spread = {}, {}, {}, {}, {}, {}, {}, {}
-        coef, std0, inv_std0, stat_t, bn_all = {}, {}, {}, {}, {}
+        def quantize_w(w):
+            quantize(("w", w), P)
+
+        product, pre = {}, {}
 
         def multiply(q, j):
-            l, bg, c, t = q // 2, q % 2, j // 4, j % 4
-            products[(q, j)] = product_bank([P, HALF], F32)
+            product[(q, j)] = bank_of("product")
+            w, r = ("w", BLOCKS * (q // 2) + j), ("h", q % 2)
             for g in range(2):
                 nc.tensor.matmul_mx(
-                    out=products[(q, j)][:],
-                    lhsT=w_codes[2 * l + c][:, g, t * P : (t + 1) * P].bitcast(FP8X4),
-                    lhsT_scale=w_scales[2 * l + c][:, g, t * P : (t + 1) * P],
-                    rhs=h_codes[bg][:, g, :].bitcast(FP8X4),
-                    rhs_scale=h_scales[bg][:, g, :],
+                    out=flat(product[(q, j)]),
+                    lhsT=codes[w][:, g, :].bitcast(FP8X4),
+                    lhsT_scale=scales[w][:, g, :],
+                    rhs=codes[r][:, g, :].bitcast(FP8X4),
+                    rhs_scale=scales[r][:, g, :],
                     start=(g == 0),
                     stop=(g == 1),
                 )
@@ -165,274 +181,203 @@ def tile_advancedliquidneuralnetwork_pa_kernel(tc, h, W_liq_bytes, W_liq_scale, 
         def add_h(q, j):
             l, bg, c, t = q // 2, q % 2, j // 4, j % 4
             if j == 0:
-                pre_t[q] = work.tile([P, 8, HALF], F32, name="pre_t", tag="pre_t", bufs=QUADS)
+                pre[q] = const.tile([P, BLOCKS, HALF], F32, name="pre%d" % q)
             nc.vector.scalar_tensor_tensor(
-                out=pre_t[q][:, j, :],
-                in0=products[(q, j)][:],
-                scalar=cols[:, 0, 8 * l + j : 8 * l + j + 1],
+                out=pre[q][:, j, :],
+                in0=flat(product[(q, j)]),
+                scalar=b_cols[:, l, c, t : t + 1],
                 in1=lined[("h", bg)][:, c, :, t],
                 op0=ALU.add,
                 op1=ALU.add,
             )
 
-        def to_rows(q, u):
-            for c in range(2):
-                banks[(q, u, c)] = row_bank([P, HALF], F32)
-                for t in range(4):
-                    nc.tensor.transpose(out=banks[(q, u, c)][:, t * P : (t + 1) * P], in_=pre_t[q][:, 4 * c + t, u * P : (u + 1) * P], identity=ident_f32[:])
+        rows, bn_parts, bn_both, half_mean, neg_mean, squares, total, std, inv_std, ratio = {}, {}, {}, {}, {}, {}, {}, {}, {}, {}
+        coef = {}
+        for bg in range(GROUPS):
+            coef[bg] = const.tile([P, TILES, 6], F32, name="coef%d" % bg)
 
-        def stats(q, u):
-            l, bg = q // 2, q % 2
-            if u == 0 and q not in OPT["sum_pe"]:
-                part_sum[q] = small.tile([P, 4], F32, name="part_sum")
-                sq_sum[q] = small.tile([P, 8], F32, name="sq_sum")
-                if l == 0:
-                    coef[bg] = const.tile([P, 4, 6], F32, name="coef%d" % bg)
-                else:
-                    neg_mean[q] = small.tile([P, 4], F32, name="neg_mean")
-            mean_col = coef[bg][:, u, 0:1] if l == 0 else neg_mean[q][:, u : u + 1]
-            if q in OPT["bnq"]:
-                if u == 0:
-                    bn_all[q] = small.tile([P, 4, 2], F32, name="bn_all")
-                bn_st = small.tile([P, 2, 6], F32, name="bn_st")
-                for c in range(2):
-                    nc.vector.bn_stats(out=bn_st[:, c, :], in_=banks[(q, u, c)][:])
-                nc.vector.bn_aggr(out=bn_all[q][:, u, :], in_=bn_st[:].rearrange("p c s -> p (c s)"))
-                return
-            if (q, u) in OPT["bn"]:
-                bn_st = small.tile([P, 2, 6], F32, name="bn_st")
-                for c in range(2):
-                    nc.vector.bn_stats(out=bn_st[:, c, :], in_=banks[(q, u, c)][:])
-                bn_mv = small.tile([P, 2], F32, name="bn_mv")
-                nc.vector.bn_aggr(out=bn_mv[:], in_=bn_st[:].rearrange("p c s -> p (c s)"))
-                nc.vector.tensor_scalar_mul(out=mean_col, in0=bn_mv[:, 0:1], scalar1=-1.0)
-                nc.vector.tensor_scalar_mul(out=sq_sum[q][:, 2 * u : 2 * u + 2], in0=bn_mv[:, 1:2].to_broadcast([P, 2]), scalar1=H / 2.0)
-                return
-            if q not in OPT["sum_pe"]:
-                junk = work.tile([P, HALF], BF16, name="junk", tag="junk", bufs=2)
-                nc.scalar.activation(out=junk[:], in_=banks[(q, u, 0)][:], func=ACT.Copy, scale=-1.0 / (H * HALF), accum_out=part_sum[q][:, u : u + 1])
-                junk = work.tile([P, HALF], BF16, name="junk", tag="junk", bufs=2)
-                nc.scalar.activation(out=junk[:], in_=banks[(q, u, 1)][:], func=ACT.Identity, scale=-1.0 / H, bias=part_sum[q][:, u : u + 1], accum_out=mean_col)
-            for c in range(2):
-                junk = work.tile([P, HALF], BF16, name="junk", tag="junk", bufs=2)
-                nc.scalar.activation(out=junk[:], in_=banks[(q, u, c)][:], func=ACT.Square, bias=mean_col, scale=1.0, accum_out=sq_sum[q][:, 2 * u + c : 2 * u + c + 1])
+        def open_sums(q):
+            half_mean[q] = small.tile([P, TILES], F32, name="half_mean")
+            squares[q] = small.tile([P, TILES, 2], F32, name="squares")
+            if q < GROUPS:
+                neg_mean[q] = coef[q][:, :, 0]
+            else:
+                neg_mean[q] = small.tile([P, TILES], F32, name="neg_mean")[:]
 
-        def finish_stats(q):
-            l, bg = q // 2, q % 2
-            total = small.tile([P, 4], F32, name="total")
-            var_eps = small.tile([P, 4], F32, name="var_eps")
-            with tc.high_priority():
-                if q in OPT["bnq"]:
-                    nc.vector.tensor_scalar_add(out=var_eps[:], in0=bn_all[q][:, :, 1], scalar1=LN_EPS)
-                    nc.vector.tensor_scalar_mul(out=(coef[bg][:, :, 0] if l == 0 else neg_mean[q][:]), in0=bn_all[q][:, :, 0], scalar1=-1.0)
-                else:
-                    nc.vector.tensor_reduce(out=total[:], in_=sq_sum[q][:].rearrange("p (u c) -> p u c", c=2), axis=AX.X, op=ALU.add)
-                    nc.vector.tensor_scalar(out=var_eps[:], in0=total[:], scalar1=1.0 / H, scalar2=LN_EPS, op0=ALU.mult, op1=ALU.add)
-                if l == 0:
-                    std0[bg] = const.tile([P, 4], F32, name="std0_%d" % bg)
-                    inv_std0[bg] = const.tile([P, 4], F32, name="inv_std0_%d" % bg)
-                    nc.scalar.activation(out=std0[bg][:], in_=var_eps[:], func=ACT.Sqrt)
-                    nc.vector.reciprocal(out=inv_std0[bg][:], in_=std0[bg][:])
-                    nc.vector.tensor_copy(out=coef[bg][:, :, 3:6], in_=std0[bg][:].unsqueeze(2).to_broadcast([P, 4, 3]))
-                else:
-                    std = small.tile([P, 4], F32, name="std")
-                    inv_std = small.tile([P, 4], F32, name="inv_std")
-                    rho[q] = small.tile([P, 4], F32, name="rho")
-                    nc.scalar.activation(out=std[:], in_=var_eps[:], func=ACT.Sqrt)
-                    nc.vector.reciprocal(out=inv_std[:], in_=std[:])
-                    nc.vector.tensor_tensor(out=rho[q][:], in0=inv_std[:], in1=std0[bg][:], op=ALU.mult)
-                    nc.vector.tensor_tensor(out=coef[bg][:, :, l], in0=neg_mean[q][:], in1=rho[q][:], op=ALU.mult)
-                    spread[q] = spread_bank([P, HALF], F32)
-                    for u in range(4):
-                        nc.tensor.matmul(
-                            out=spread[q][:, u * P : (u + 1) * P],
-                            lhsT=rho[q][:, u : u + 1].to_broadcast([P, P]),
-                            rhs=ident_f32[:],
-                            is_transpose=True,
-                            start=True,
-                            stop=True,
-                        )
+        def to_rows(q, u, c):
+            rows[(q, u, c)] = bank_of("row")
+            for t in range(4):
+                turn(rows[(q, u, c)][:, t, :], pre[q][:, 4 * c + t, u * P : (u + 1) * P])
 
-        def split_coef(bg):
-            rest = coef[bg]
-            with tc.high_priority():
-                for s in range(PIECES):
-                    piece = stat_rows[bg][:, :, 6 * s : 6 * s + 6]
-                    nc.vector.tensor_copy(out=piece, in_=rest[:])
-                    if s + 1 < PIECES:
-                        smaller = small.tile([P, 4, 6], F32, name="smaller")
-                        nc.vector.tensor_tensor(out=smaller[:], in0=rest[:], in1=piece, op=ALU.subtract)
-                        rest = smaller
-                bank = turn_bank([P, 4, P], BF16)
-                for u in range(4):
-                    nc.tensor.transpose(out=bank[:, u, :], in_=stat_rows[bg][:, u, :], identity=ident_bf16[:])
-                stat_t[bg] = const.tile([P, 4, P], BF16, name="stat_t%d" % bg)
-                nc.scalar.copy(out=stat_t[bg][:], in_=bank[:])
+        def sum_half(q, u, c):
+            junk = work.tile([P, HALF], BF16, name="junk", tag="junk", bufs=2)
+            bank = flat(rows[(q, u, c)])
+            if c == 0:
+                nc.scalar.activation(out=junk[:], in_=bank, func=ACT.Copy, scale=-1.0 / (H * HALF), accum_out=half_mean[q][:, u : u + 1])
+            else:
+                nc.scalar.activation(out=junk[:], in_=bank, func=ACT.Identity, scale=-1.0 / H, bias=half_mean[q][:, u : u + 1], accum_out=neg_mean[q][:, u : u + 1])
+
+        def square_half(q, u, c):
+            junk = work.tile([P, HALF], BF16, name="junk", tag="junk", bufs=2)
+            nc.scalar.activation(out=junk[:], in_=flat(rows[(q, u, c)]), func=ACT.Square, bias=neg_mean[q][:, u : u + 1], scale=1.0, accum_out=squares[q][:, u, c : c + 1])
+
+        def bn_half(q, u, c):
+            if c == 0:
+                bn_parts[(q, u)] = small.tile([P, 2, 6], F32, name="bn_parts")
+            nc.vector.bn_stats(out=bn_parts[(q, u)][:, c, :], in_=flat(rows[(q, u, c)]))
+
+        def bn_join(q, u):
+            bn_both[(q, u)] = small.tile([P, 2], F32, name="bn_both")
+            nc.vector.bn_aggr(out=bn_both[(q, u)][:], in_=bn_parts[(q, u)][:].rearrange("p c s -> p (c s)"))
+
+        def bn_end(q, u):
+            nc.vector.tensor_scalar_mul(out=neg_mean[q][:, u : u + 1], in0=bn_both[(q, u)][:, 0:1], scalar1=-1.0)
+            nc.vector.tensor_scalar_mul(out=squares[q][:, u, :], in0=bn_both[(q, u)][:, 1:2].to_broadcast([P, 2]), scalar1=H / 2.0)
+
+        def add_squares(q):
+            total[q] = small.tile([P, TILES], F32, name="total")
+            nc.vector.tensor_tensor(out=total[q][:], in0=squares[q][:, :, 0], in1=squares[q][:, :, 1], op=ALU.add)
+
+        def take_root(q):
+            std[q] = const.tile([P, TILES], F32, name="std%d" % q)
+            nc.scalar.activation(out=std[q][:], in_=total[q][:], func=ACT.Sqrt, scale=1.0 / H, bias=eps_col[:])
+
+        def invert(q):
+            inv_std[q] = const.tile([P, TILES], F32, name="inv_std%d" % q)
+            nc.vector.reciprocal(out=inv_std[q][:], in_=std[q][:])
+
+        def scale_ratio(q):
+            bg = q % 2
+            if q < GROUPS:
+                nc.vector.tensor_copy(out=coef[bg][:, :, 3:6], in_=std[q][:].unsqueeze(2).to_broadcast([P, TILES, 3]))
+            else:
+                ratio[q] = small.tile([P, TILES], F32, name="ratio")
+                nc.vector.tensor_tensor(out=ratio[q][:], in0=inv_std[q][:], in1=std[bg][:], op=ALU.mult)
+                nc.vector.tensor_tensor(out=coef[bg][:, :, q // 2], in0=neg_mean[q], in1=ratio[q][:], op=ALU.mult)
+
+        spread, coef_rest, coef_bank, coef_t, closing = {}, {}, {}, {}, {}
+
+        def spread_ratio(q):
+            spread[q] = bank_of("turn")
+            for u in range(TILES):
+                turn(spread[q][:, u, :], ratio[q][:, u : u + 1].to_broadcast([P, P]))
 
         def apply_gain(q, j):
-            l = q // 2
-            gain = cols[:, 1, 8 * l + j : 8 * l + j + 1]
-            if l == 0 and OPT["merge01"]:
-                nc.vector.scalar_tensor_tensor(out=pre_t[q + 2][:, j, :], in0=pre_t[q][:, j, :], scalar=gain, in1=pre_t[q + 2][:, j, :], op0=ALU.mult, op1=ALU.add)
-            elif l == 0 and q in OPT["t0g"]:
-                nc.gpsimd.tensor_scalar(out=pre_t[q][:, j, :], in0=pre_t[q][:, j, :], scalar1=gain, scalar2=0.0, op0=ALU.mult, op1=ALU.add)
-            elif l == 0 and q in OPT["t0s"]:
-                nc.scalar.activation(out=pre_t[q][:, j, :], in_=pre_t[q][:, j, :], func=ACT.Copy, scale=gain)
-            elif l == 0:
-                nc.vector.tensor_scalar_mul(out=pre_t[q][:, j, :], in0=pre_t[q][:, j, :], scalar1=gain)
-            else:
-                nc.vector.scalar_tensor_tensor(out=pre_t[q][:, j, :], in0=pre_t[q][:, j, :], scalar=gain, in1=spread[q][:], op0=ALU.mult, op1=ALU.mult)
+            gain = g_cols[:, q // 2, j // 4, j % 4 : j % 4 + 1]
+            nc.vector.scalar_tensor_tensor(out=pre[q][:, j, :], in0=pre[q][:, j, :], scalar=gain, in1=flat(spread[q]), op0=ALU.mult, op1=ALU.mult)
 
-        def finish(bg, u, c):
-            tags = OPT["fin_tags"][bg]
-            tag = tags[(4 * c + u) % len(tags)]
-            bank = {"turn": turn_bank, "product": product_bank, "row": row_bank, "spread": spread_bank}[tag]([P, HALF], F32)
-            first = OPT["coef_first"]
-            if first:
-                nc.tensor.matmul(out=bank[:], lhsT=stat_t[bg][:, u, :], rhs=vec_perm[:, c, :, :].rearrange("p t m -> p (t m)"), start=True, stop=False)
-            ls = [1, 2] if OPT["merge01"] else [0, 1, 2]
-            for l in ls:
+        def join_branch_0(bg, j):
+            gain = g_cols[:, 0, j // 4, j % 4 : j % 4 + 1]
+            both = pre[2 + bg][:, j, :]
+            nc.vector.scalar_tensor_tensor(out=both, in0=pre[bg][:, j, :], scalar=gain, in1=both, op0=ALU.mult, op1=ALU.add)
+
+        def split_coef(bg):
+            first, second, third = (coef_rows[bg][:, :, 6 * s : 6 * s + 6] for s in range(PIECES))
+            rest = small.tile([P, TILES, 6], F32, name="rest")
+            nc.vector.tensor_copy(out=first, in_=coef[bg][:])
+            nc.vector.tensor_tensor(out=second, in0=coef[bg][:], in1=first, op=ALU.subtract)
+            nc.vector.tensor_tensor(out=rest[:], in0=coef[bg][:], in1=first, op=ALU.subtract)
+            nc.vector.tensor_tensor(out=third, in0=rest[:], in1=second, op=ALU.subtract)
+
+        def turn_coef(bg):
+            coef_bank[bg] = bank_of("turn", BF16)
+            for u in range(TILES):
+                nc.tensor.transpose(out=coef_bank[bg][:, u, :], in_=coef_rows[bg][:, u, :], identity=ident_bf16[:])
+
+        def copy_coef(bg):
+            coef_t[bg] = const.tile([P, TILES, P], BF16, name="coef_t%d" % bg)
+            nc.scalar.copy(out=coef_t[bg][:], in_=coef_bank[bg][:])
+
+        def close(bg, u, c, tag):
+            closing[(bg, u, c)] = bank_of(tag)
+            for l in (1, 2):
                 for t in range(4):
-                    nc.tensor.matmul(
-                        out=bank[:, t * P : (t + 1) * P],
-                        lhsT=pre_t[2 * l + bg][:, 4 * c + t, u * P : (u + 1) * P],
-                        rhs=ident_f32[:],
-                        is_transpose=True,
-                        start=(not first and l == ls[0] and t == 0),
-                        stop=(first and l == L - 1 and t == 3),
-                    )
-            if not first:
-                nc.tensor.matmul(out=bank[:], lhsT=stat_t[bg][:, u, :], rhs=vec_perm[:, c, :, :].rearrange("p t m -> p (t m)"), start=False, stop=True)
-            if (4 * c + u) % 2 == 0:
-                result = work.tile([P, HALF], F32, name="h_rows", tag="h_rows", bufs=4)
+                    turn(closing[(bg, u, c)][:, t, :], pre[GROUPS * l + bg][:, 4 * c + t, u * P : (u + 1) * P], start=(l == 1 and t == 0), stop=False)
+            vectors = vec_perm[:, c, :, :].rearrange("p t m -> p (t m)")
+            nc.tensor.matmul(out=flat(closing[(bg, u, c)]), lhsT=coef_t[bg][:, u, :], rhs=vectors, start=False, stop=True)
+
+        def take_out(bg, u, c, engine):
+            tag = "h_rows" if u % 2 == 0 else "w_bf16"
+            result = work.tile([P, HALF], F32, name=tag, tag=tag, bufs=4)
+            features = result[:].rearrange("p (m t) -> p m t", t=4)
+            closed = closing[(bg, u, c)][:].rearrange("p t m -> p m t")
+            divisor = inv_std[bg][:, u : u + 1]
+            if engine == "vector":
+                nc.vector.tensor_scalar_mul(out=features, in0=closed, scalar1=divisor)
             else:
-                result = work.tile([P, HALF], F32, name="w_bf16", tag="w_bf16", bufs=OPT["wbf"])
-            if u in (OPT["vfinal1"] if bg == 1 else OPT["vfinal"]):
-                nc.vector.tensor_scalar_mul(
-                    out=result[:].rearrange("p (m t) -> p m t", t=4),
-                    in0=bank[:].rearrange("p (t m) -> p m t", t=4),
-                    scalar1=inv_std0[bg][:, u : u + 1],
-                )
-            else:
-                nc.scalar.activation(
-                    out=result[:].rearrange("p (m t) -> p m t", t=4),
-                    in_=bank[:].rearrange("p (t m) -> p m t", t=4),
-                    func=ACT.Copy,
-                    scale=inv_std0[bg][:, u : u + 1],
-                )
-            r0 = (4 * bg + u) * P
-            nc.sync.dma_start(out=out[r0 : r0 + P, c * HALF : (c + 1) * HALF], in_=result[:])
+                nc.scalar.activation(out=features, in_=closed, func=ACT.Copy, scale=divisor)
+            row = (TILES * bg + u) * P
+            nc.sync.dma_start(out=out[row : row + P, c * HALF : (c + 1) * HALF], in_=result[:])
 
-        def products_of(q, blocks):
-            for j in blocks:
-                multiply(q, j)
-                add_h(q, j)
+        plan = []
 
-        def prepare_w(x):
-            for w in range(4 * x, 4 * x + 4):
-                widen(w)
-                turn_w(w)
-            quantize_w(x)
+        def at(step, stage, *args):
+            plan.append((step, len(plan), stage, args))
 
-        def means_by_pe(q):
-            l, bg = q // 2, q % 2
-            part_sum[q] = small.tile([P, 4], F32, name="part_sum")
-            sq_sum[q] = small.tile([P, 8], F32, name="sq_sum")
-            if l == 0:
-                coef[bg] = const.tile([P, 4, 6], F32, name="coef%d" % bg)
-            else:
-                neg_mean[q] = small.tile([P, 4], F32, name="neg_mean")
-            bank = {"turn": turn_bank, "spread": spread_bank, "row": row_bank}[OPT["sum_tag"]]([P, 4, P], F32)
-            for u in range(4):
-                for j in range(8):
-                    nc.tensor.matmul(out=bank[:, u, :], lhsT=pre_t[q][:, j, u * P : (u + 1) * P], rhs=ident_f32[:], is_transpose=True, start=(j == 0), stop=(j == 7))
-            cols4 = coef[bg][:, :, 0] if l == 0 else neg_mean[q][:]
-            if OPT["sum_red"] == "V":
-                nc.vector.tensor_reduce(out=part_sum[q][:], in_=bank[:], axis=AX.X, op=ALU.add)
-                nc.vector.tensor_scalar_mul(out=cols4, in0=part_sum[q][:], scalar1=-1.0 / H)
-            else:
-                for u in range(4):
-                    junk = work.tile([P, HALF], BF16, name="junk", tag="junk", bufs=2)
-                    nc.scalar.activation(out=junk[:, 0:P], in_=bank[:, u, :], func=ACT.Copy, scale=-1.0 / H, accum_out=(coef[bg][:, u, 0:1] if l == 0 else neg_mean[q][:, u : u + 1]))
+        at(-21, spread_scales)
+        for t in range(4):
+            at(-20 + t, widen, t)
+            at(-20 + t, turn_h, t)
+            at(-20 + t, line_h, t)
+            at(-16 + t, turn_w, t, "row")
+            at(-16 + t, line_w, t)
+        at(-12, quantize_h, 0)
+        for t in range(4):
+            at(-11, quantize_w, t)
 
-        def sums_of(q):
-            if q in OPT["sum_pe"]:
-                means_by_pe(q)
-            for u in range(4):
-                to_rows(q, u)
-                stats(q, u)
-            finish_stats(q)
+        for n in range(BLOCKS * QUADS):
+            at(n, multiply, n // BLOCKS, n % BLOCKS)
+            at(n, add_h, n // BLOCKS, n % BLOCKS)
 
-        def gains_of(q):
-            for j in range(8):
-                apply_gain(q, j)
+        for w in range(4, BLOCKS * L):
+            step = w - LEAD if w < BLOCKS else 2 * w - 7 - LEAD
+            at(step + 0.1, widen, w)
+            at(step + 0.2, turn_w, w, "turn")
+            at(step + LEAD - 1 + 0.3, line_w, w)
+            at(step + LEAD - 0.1, quantize_w, w)
 
-        def last_of(bg):
-            for c in range(2):
-                for t in range(4):
-                    apply_gain(4 + bg, 4 * c + t)
-                for u in range(4):
-                    finish(bg, u, c)
-
-        def perm():
-            nc.scalar.copy(out=vec_perm[:], in_=vec_rows[:].rearrange("p (c m t) -> p c t m", c=2, t=4))
-
-        for w in range(4):
-            turn_h(w)
-            widen(w)
-            turn_w(w)
-        quantize_h(0)
-        quantize_w(0)
-        products_of(0, range(4))
-        prepare_w(1)
-        products_of(0, range(4, 8))
         for i in range(4, 8):
-            turn_h(i)
-        quantize_h(1)
-        if OPT["order"] == "l":
-            products_of(1, range(8))
-            perm()
-            for l in range(L):
-                if l > 0:
-                    products_of(2 * l, range(8))
-                    products_of(2 * l + 1, range(8))
-                if l + 1 < L:
-                    prepare_w(2 * l + 2)
-                    prepare_w(2 * l + 3)
-                for bg in range(2):
-                    sums_of(2 * l + bg)
-                    if l == L - 1:
-                        split_coef(bg)
-            if OPT["merge01"]:
-                for q in (2, 3, 0, 1):
-                    gains_of(q)
-            else:
-                for q in range(4):
-                    gains_of(q)
-            for bg in range(2):
-                last_of(bg)
-        elif OPT["order"] == "r":
-            perm()
-            prepare_w(2)
-            prepare_w(3)
-            sums_of(0)
-            products_of(2, range(8))
-            prepare_w(4)
-            prepare_w(5)
-            sums_of(2)
-            products_of(4, range(8))
-            sums_of(4)
-            split_coef(0)
-            products_of(1, range(8))
-            sums_of(1)
-            products_of(3, range(8))
-            sums_of(3)
-            products_of(5, range(8))
-            for q in ((2, 0) if OPT["merge01"] else (0, 2)):
-                gains_of(q)
-            last_of(0)
-            sums_of(5)
-            split_coef(1)
-            for q in ((3, 1) if OPT["merge01"] else (1, 3)):
-                gains_of(q)
-            last_of(1)
+            at(i - 1 + 0.2, turn_h, i)
+            at(i - 1 + 0.3, line_h, i)
+        at(7.5, quantize_h, 1)
+        at(8, order_vectors)
+
+        for q in range(QUADS):
+            first = BLOCKS * (q + 1)
+            at(first - 0.2, open_sums, q)
+            for u in range(TILES):
+                step = first + 2 * u
+                at(step - 0.1, to_rows, q, u, 0)
+                at(step + 0.9, to_rows, q, u, 1)
+                if (q, u) in VECTOR_SUMS:
+                    at(step + 1, bn_half, q, u, 0)
+                    at(step + 2, bn_half, q, u, 1)
+                    at(step + 2.5, bn_join, q, u)
+                    at(step + 3, bn_end, q, u)
+                else:
+                    at(step + 1, sum_half, q, u, 0)
+                    at(step + 2, sum_half, q, u, 1)
+                    at(step + 2.5, square_half, q, u, 0)
+                    at(step + 3, square_half, q, u, 1)
+            known = first + BLOCKS + 2
+            for stage in (add_squares, take_root, invert, scale_ratio):
+                at(known, stage, q)
+            gains = known + 6
+            if q >= GROUPS:
+                at(max(known, 37), spread_ratio, q)
+                for j in range(BLOCKS):
+                    at(gains + j, apply_gain, q, j)
+            if q >= 2 * GROUPS:
+                bg = q % 2
+                for stage in (split_coef, turn_coef, copy_coef):
+                    at(known + 1, stage, bg)
+                for j in range(BLOCKS):
+                    at(gains + j - 0.5, join_branch_0, bg, j)
+                for c in range(2):
+                    for u in range(TILES):
+                        step = gains + 4 * c + 4 + u
+                        at(step, close, bg, u, c, ("product", "row", "row")[(4 * c + u) % 3])
+                        at(step + 12, take_out, bg, u, c, "vector" if bg == 1 and u % 2 == 1 else "scalar")
+
+        for step, place, stage, args in sorted(plan):
+            stage(*args)

@@ -23,7 +23,7 @@ BLOCKS = 8
 QUADS = GROUPS * L
 PIECES = 3
 BANKS = {"product": 2, "turn": 2, "row": 4}
-LEAD = 3
+LEAD = 5
 VECTOR_SUMS = ((1, 3), (3, 3))
 
 
@@ -62,13 +62,13 @@ def tile_advancedliquidneuralnetwork_pa_kernel(tc, h, W_liq_bytes, W_liq_scale, 
         for i in range(4, 8):
             load_h(i)
         load_w(2)
-        g_cols = const.tile([P, L, 2, 4], BF16, name="g_cols")
-        nc.sync.dma_start(out=g_cols[:], in_=g_liq.rearrange("l (c p t) -> p l c t", c=2, t=4))
         vec_rows = const.tile([P, H], BF16, name="vec_rows")
         nc.vector.memset(vec_rows[:], 0.0)
         for s in range(PIECES):
             nc.sync.dma_start(out=vec_rows[6 * s : 6 * s + 3, :], in_=g_liq)
             nc.sync.dma_start(out=vec_rows[6 * s + 3 : 6 * s + 6, :], in_=beta_liq)
+        g_cols = const.tile([P, L, 2, 4], BF16, name="g_cols")
+        nc.sync.dma_start(out=g_cols[:], in_=g_liq.rearrange("l (c p t) -> p l c t", c=2, t=4))
         for x in range(3, 6):
             load_w(x)
 
@@ -337,10 +337,10 @@ def tile_advancedliquidneuralnetwork_pa_kernel(tc, h, W_liq_bytes, W_liq_scale, 
             at(step + LEAD - 0.1, quantize_w, w)
 
         for i in range(4, 8):
-            at(i - 1 + 0.2, turn_h, i)
-            at(i - 1 + 0.3, line_h, i)
+            at(i - 2 + 0.2, turn_h, i)
+            at(i - 2 + 0.3, line_h, i)
         at(7.5, quantize_h, 1)
-        at(8, order_vectors)
+        at(16, order_vectors)
 
         for q in range(QUADS):
             first = BLOCKS * (q + 1)

from contextlib import ExitStack

import concourse.mybir as mybir
from concourse.masks import make_identity

B, H, L = 1024, 1024, 3
LN_EPS = 1e-5

F32 = mybir.dt.float32
BF16 = mybir.dt.bfloat16
U32 = mybir.dt.uint32
U8 = mybir.dt.uint8
FP8 = mybir.dt.float8_e4m3fn
FP8X4 = mybir.dt.float8_e4m3fn_x4
ALU = mybir.AluOpType
ACT = mybir.ActivationFunctionType

P = 128
HALF = 512
GROUPS = 2
TILES = 4
BLOCKS = 8
QUADS = GROUPS * L
PIECES = 3
BANKS = {"product": 2, "turn": 2, "row": 4}
LEAD = 5
VECTOR_SUMS = ((1, 3), (3, 3))


def tile_advancedliquidneuralnetwork_pa_kernel(tc, h, W_liq_bytes, W_liq_scale, b_liq, g_liq, beta_liq, out):
    nc = tc.nc
    with ExitStack() as ctx:
        const = ctx.enter_context(tc.tile_pool(name="const", bufs=1))
        work = ctx.enter_context(tc.tile_pool(name="work", bufs=2))
        small = ctx.enter_context(tc.tile_pool(name="small", bufs=8))
        psum = ctx.enter_context(tc.psum_pool(name="psum", bufs=2))

        scale_cols = const.tile([P, 2, 4], F32, name="scale_cols")
        nc.scalar.dma_start(out=scale_cols[:], in_=W_liq_scale.rearrange("a b (c p m) -> (a b p) c m", c=2, m=4))

        w_view = W_liq_bytes.rearrange("l (c m t) k -> l c m t k", c=2, t=4)
        h_view = h.rearrange("(i p) k -> i p k", p=P)
        w_bytes, h_rows = {}, {}

        def load_w(x):
            w_bytes[x] = work.tile([P, 4, H], U8, name="w_bytes", tag="w_bytes", bufs=3)
            if x == 0:
                for t in range(4):
                    nc.sync.dma_start(out=w_bytes[x][:, t, :], in_=w_view[0, 0, :, t, :])
                    load_h(t)
            else:
                nc.sync.dma_start(out=w_bytes[x][:], in_=w_view[x // 2, x % 2])

        def load_h(i):
            h_rows[i] = work.tile([P, H], BF16, name="h_rows", tag="h_rows", bufs=4)
            nc.sync.dma_start(out=h_rows[i][:], in_=h_view[i])

        load_w(0)
        load_w(1)
        b_cols = const.tile([P, L, 2, 4], BF16, name="b_cols")
        nc.sync.dma_start(out=b_cols[:], in_=b_liq.rearrange("l (c p t) -> p l c t", c=2, t=4))
        for i in range(4, 8):
            load_h(i)
        load_w(2)
        vec_rows = const.tile([P, H], BF16, name="vec_rows")
        nc.vector.memset(vec_rows[:], 0.0)
        for s in range(PIECES):
            nc.sync.dma_start(out=vec_rows[6 * s : 6 * s + 3, :], in_=g_liq)
            nc.sync.dma_start(out=vec_rows[6 * s + 3 : 6 * s + 6, :], in_=beta_liq)
        g_cols = const.tile([P, L, 2, 4], BF16, name="g_cols")
        nc.sync.dma_start(out=g_cols[:], in_=g_liq.rearrange("l (c p t) -> p l c t", c=2, t=4))
        for x in range(3, 6):
            load_w(x)

        one = const.tile([P, 1], F32, name="one")
        nc.vector.memset(one[:], 1.0)
        eps_col = const.tile([P, 1], F32, name="eps_col")
        nc.vector.tensor_scalar_mul(out=eps_col[:], in0=one[:], scalar1=LN_EPS)
        one_root = const.tile([P, 1], F32, name="one_root")
        nc.scalar.activation(out=one_root[:], in_=one[:], func=ACT.Sqrt)
        ident_f32 = const.tile([P, P], F32, name="ident_f32")
        make_identity(nc, ident_f32[:])
        ident_bf16 = const.tile([P, P], BF16, name="ident_bf16")
        make_identity(nc, ident_bf16[:])
        coef_rows = {}
        for bg in range(GROUPS):
            coef_rows[bg] = const.tile([P, TILES, P], BF16, name="coef_rows%d" % bg)
            nc.vector.memset(coef_rows[bg][:], 0.0)
        scale_all = const.tile([P, H], F32, name="scale_all")
        vec_perm = const.tile([P, 2, 4, P], BF16, name="vec_perm")

        def bank_of(tag, dtype=F32):
            return psum.tile([P, 4, P], dtype, name=tag, tag=tag, bufs=BANKS[tag])

        def flat(bank):
            return bank[:].rearrange("p a b -> p (a b)")

        def spread_scales():
            for c in range(2):
                bank = bank_of("product")
                for m in range(4):
                    turn(bank[:, m, :], scale_cols[:, c, m : m + 1].to_broadcast([P, P]))
                half = scale_all[:, c * HALF : (c + 1) * HALF].rearrange("q (p m) -> q p m", m=4)
                if c == 0:
                    nc.vector.tensor_copy(out=half, in_=bank[:].rearrange("q m p -> q p m"))
                else:
                    nc.scalar.copy(out=half, in_=bank[:].rearrange("q m p -> q p m"))

        def order_vectors():
            nc.scalar.copy(out=vec_perm[:], in_=vec_rows[:].rearrange("p (c m t) -> p c t m", c=2, t=4))

        def turn(bank, block, start=True, stop=True):
            nc.tensor.matmul(out=bank, lhsT=block, rhs=ident_f32[:], is_transpose=True, start=start, stop=stop)

        turned, lined, codes, scales, w_bf16 = {}, {}, {}, {}, {}

        def turn_words(key, rows, tag):
            words = rows.bitcast(F32)
            turned[key] = bank_of(tag)
            for g in range(2):
                for e in range(2):
                    turn(turned[key][:, 2 * g + e, :], words[:, 256 * g + e : 256 * (g + 1) : 2])

        def line_up(key, dst, first_row):
            words = dst[:].rearrange("p g r t -> p (g r t)").bitcast(F32).rearrange("p (g r e) -> p g r e", g=2, e=2)
            nc.scalar.copy(out=words[:, :, first_row : first_row + P, :], in_=turned[key][:].rearrange("p (g e) r -> p g r e", e=2))

        def quantize(key, rows):
            name = "%s%d" % key
            codes[key] = const.tile([P, 2, rows], U32, name="codes_" + name, align_bytes=64)
            scales[key] = const.tile([P, 2, rows], U8, name="scales_" + name, align_bytes=64)
            nc.vector.quantize_mx(
                out=codes[key][:].rearrange("p g r -> p (g r)").bitcast(FP8X4),
                scales=scales[key][:].rearrange("p g r -> p (g r)"),
                in_=lined[key][:].rearrange("p g r t -> p (g r t)"),
            )

        def turn_h(i):
            turn_words(("row tile", i), h_rows[i][:], "turn")

        def line_h(i):
            key = ("h", i // TILES)
            if i % TILES == 0:
                lined[key] = const.tile([P, 2, HALF, 4], BF16, name="lined_h%d" % key[1], align_bytes=64)
            line_up(("row tile", i), lined[key], i % TILES * P)

        def quantize_h(bg):
            quantize(("h", bg), HALF)

        def widen(w):
            w_bf16[w] = work.tile([P, H], BF16, name="w_bf16", tag="w_bf16", bufs=4)
            for part in (slice(0, HALF), slice(HALF, H)) if w == 0 else (slice(0, H),):
                nc.vector.tensor_tensor(out=w_bf16[w][:, part], in0=w_bytes[w // 4][:, w % 4, part].bitcast(FP8), in1=scale_all[:, part], op=ALU.mult)

        def turn_w(w, tag):
            turn_words(("w", w), w_bf16[w][:], tag)

        def line_w(w):
            lined[("w", w)] = work.tile([P, 2, P, 4], BF16, name="lined_w", tag="lined_w", bufs=8, align_bytes=64)
            line_up(("w", w), lined[("w", w)], 0)

        def quantize_w(w):
            quantize(("w", w), P)

        product, pre = {}, {}

        def multiply(q, j):
            product[(q, j)] = bank_of("product")
            w, r = ("w", BLOCKS * (q // 2) + j), ("h", q % 2)
            for g in range(2):
                nc.tensor.matmul_mx(
                    out=flat(product[(q, j)]),
                    lhsT=codes[w][:, g, :].bitcast(FP8X4),
                    lhsT_scale=scales[w][:, g, :],
                    rhs=codes[r][:, g, :].bitcast(FP8X4),
                    rhs_scale=scales[r][:, g, :],
                    start=(g == 0),
                    stop=(g == 1),
                )

        def add_h(q, j):
            l, bg, c, t = q // 2, q % 2, j // 4, j % 4
            if j == 0:
                pre[q] = const.tile([P, BLOCKS, HALF], F32, name="pre%d" % q)
            nc.vector.scalar_tensor_tensor(
                out=pre[q][:, j, :],
                in0=flat(product[(q, j)]),
                scalar=b_cols[:, l, c, t : t + 1],
                in1=lined[("h", bg)][:, c, :, t],
                op0=ALU.add,
                op1=ALU.add,
            )

        rows, bn_parts, bn_both, half_mean, neg_mean, squares, total, std, inv_std, ratio = {}, {}, {}, {}, {}, {}, {}, {}, {}, {}
        coef = {}
        for bg in range(GROUPS):
            coef[bg] = const.tile([P, TILES, 6], F32, name="coef%d" % bg)

        def open_sums(q):
            half_mean[q] = small.tile([P, TILES], F32, name="half_mean")
            squares[q] = small.tile([P, TILES, 2], F32, name="squares")
            if q < GROUPS:
                neg_mean[q] = coef[q][:, :, 0]
            else:
                neg_mean[q] = small.tile([P, TILES], F32, name="neg_mean")[:]

        def to_rows(q, u, c):
            rows[(q, u, c)] = bank_of("row")
            for t in range(4):
                turn(rows[(q, u, c)][:, t, :], pre[q][:, 4 * c + t, u * P : (u + 1) * P])

        def sum_half(q, u, c):
            junk = work.tile([P, HALF], BF16, name="junk", tag="junk", bufs=2)
            bank = flat(rows[(q, u, c)])
            if c == 0:
                nc.scalar.activation(out=junk[:], in_=bank, func=ACT.Copy, scale=-1.0 / (H * HALF), accum_out=half_mean[q][:, u : u + 1])
            else:
                nc.scalar.activation(out=junk[:], in_=bank, func=ACT.Identity, scale=-1.0 / H, bias=half_mean[q][:, u : u + 1], accum_out=neg_mean[q][:, u : u + 1])

        def square_half(q, u, c):
            junk = work.tile([P, HALF], BF16, name="junk", tag="junk", bufs=2)
            nc.scalar.activation(out=junk[:], in_=flat(rows[(q, u, c)]), func=ACT.Square, bias=neg_mean[q][:, u : u + 1], scale=1.0, accum_out=squares[q][:, u, c : c + 1])

        def bn_half(q, u, c):
            if c == 0:
                bn_parts[(q, u)] = small.tile([P, 2, 6], F32, name="bn_parts")
            nc.vector.bn_stats(out=bn_parts[(q, u)][:, c, :], in_=flat(rows[(q, u, c)]))

        def bn_join(q, u):
            bn_both[(q, u)] = small.tile([P, 2], F32, name="bn_both")
            nc.vector.bn_aggr(out=bn_both[(q, u)][:], in_=bn_parts[(q, u)][:].rearrange("p c s -> p (c s)"))

        def bn_end(q, u):
            nc.vector.tensor_scalar_mul(out=neg_mean[q][:, u : u + 1], in0=bn_both[(q, u)][:, 0:1], scalar1=-1.0)
            nc.vector.tensor_scalar_mul(out=squares[q][:, u, :], in0=bn_both[(q, u)][:, 1:2].to_broadcast([P, 2]), scalar1=H / 2.0)

        def add_squares(q):
            total[q] = small.tile([P, TILES], F32, name="total")
            nc.vector.tensor_tensor(out=total[q][:], in0=squares[q][:, :, 0], in1=squares[q][:, :, 1], op=ALU.add)

        def take_root(q):
            std[q] = const.tile([P, TILES], F32, name="std%d" % q)
            nc.scalar.activation(out=std[q][:], in_=total[q][:], func=ACT.Sqrt, scale=1.0 / H, bias=eps_col[:])

        def invert(q):
            inv_std[q] = const.tile([P, TILES], F32, name="inv_std%d" % q)
            nc.vector.reciprocal(out=inv_std[q][:], in_=std[q][:])

        def scale_ratio(q):
            bg = q % 2
            if q < GROUPS:
                nc.vector.tensor_copy(out=coef[bg][:, :, 3:6], in_=std[q][:].unsqueeze(2).to_broadcast([P, TILES, 3]))
            else:
                ratio[q] = small.tile([P, TILES], F32, name="ratio")
                nc.vector.tensor_tensor(out=ratio[q][:], in0=inv_std[q][:], in1=std[bg][:], op=ALU.mult)
                nc.vector.tensor_tensor(out=coef[bg][:, :, q // 2], in0=neg_mean[q], in1=ratio[q][:], op=ALU.mult)

        spread, coef_rest, coef_bank, coef_t, closing = {}, {}, {}, {}, {}

        def spread_ratio(q):
            spread[q] = bank_of("turn")
            for u in range(TILES):
                turn(spread[q][:, u, :], ratio[q][:, u : u + 1].to_broadcast([P, P]))

        def apply_gain(q, j):
            gain = g_cols[:, q // 2, j // 4, j % 4 : j % 4 + 1]
            nc.vector.scalar_tensor_tensor(out=pre[q][:, j, :], in0=pre[q][:, j, :], scalar=gain, in1=flat(spread[q]), op0=ALU.mult, op1=ALU.mult)

        def join_branch_0(bg, j):
            gain = g_cols[:, 0, j // 4, j % 4 : j % 4 + 1]
            both = pre[2 + bg][:, j, :]
            nc.vector.scalar_tensor_tensor(out=both, in0=pre[bg][:, j, :], scalar=gain, in1=both, op0=ALU.mult, op1=ALU.add)

        def split_coef(bg):
            first, second, third = (coef_rows[bg][:, :, 6 * s : 6 * s + 6] for s in range(PIECES))
            rest = small.tile([P, TILES, 6], F32, name="rest")
            nc.vector.tensor_copy(out=first, in_=coef[bg][:])
            nc.vector.tensor_tensor(out=second, in0=coef[bg][:], in1=first, op=ALU.subtract)
            nc.vector.tensor_tensor(out=rest[:], in0=coef[bg][:], in1=first, op=ALU.subtract)
            nc.vector.tensor_tensor(out=third, in0=rest[:], in1=second, op=ALU.subtract)

        def turn_coef(bg):
            coef_bank[bg] = bank_of("turn", BF16)
            for u in range(TILES):
                nc.tensor.transpose(out=coef_bank[bg][:, u, :], in_=coef_rows[bg][:, u, :], identity=ident_bf16[:])

        def copy_coef(bg):
            coef_t[bg] = const.tile([P, TILES, P], BF16, name="coef_t%d" % bg)
            nc.scalar.copy(out=coef_t[bg][:], in_=coef_bank[bg][:])

        def close(bg, u, c, tag):
            closing[(bg, u, c)] = bank_of(tag)
            for l in (1, 2):
                for t in range(4):
                    turn(closing[(bg, u, c)][:, t, :], pre[GROUPS * l + bg][:, 4 * c + t, u * P : (u + 1) * P], start=(l == 1 and t == 0), stop=False)
            vectors = vec_perm[:, c, :, :].rearrange("p t m -> p (t m)")
            nc.tensor.matmul(out=flat(closing[(bg, u, c)]), lhsT=coef_t[bg][:, u, :], rhs=vectors, start=False, stop=True)

        def take_out(bg, u, c, engine):
            tag = "h_rows" if u % 2 == 0 else "w_bf16"
            result = work.tile([P, HALF], F32, name=tag, tag=tag, bufs=4)
            features = result[:].rearrange("p (m t) -> p m t", t=4)
            closed = closing[(bg, u, c)][:].rearrange("p t m -> p m t")
            divisor = inv_std[bg][:, u : u + 1]
            if engine == "vector":
                nc.vector.tensor_scalar_mul(out=features, in0=closed, scalar1=divisor)
            else:
                nc.scalar.activation(out=features, in_=closed, func=ACT.Copy, scale=divisor)
            row = (TILES * bg + u) * P
            nc.sync.dma_start(out=out[row : row + P, c * HALF : (c + 1) * HALF], in_=result[:])

        plan = []

        def at(step, stage, *args):
            plan.append((step, len(plan), stage, args))

        at(-21, spread_scales)
        for t in range(4):
            at(-20 + t, widen, t)
            at(-20 + t, turn_h, t)
            at(-20 + t, line_h, t)
            at(-16 + t, turn_w, t, "row")
            at(-16 + t, line_w, t)
        at(-12, quantize_h, 0)
        for t in range(4):
            at(-11, quantize_w, t)

        for n in range(BLOCKS * QUADS):
            at(n, multiply, n // BLOCKS, n % BLOCKS)
            at(n, add_h, n // BLOCKS, n % BLOCKS)

        for w in range(4, BLOCKS * L):
            step = w - LEAD if w < BLOCKS else 2 * w - 7 - LEAD
            at(step + 0.1, widen, w)
            at(step + 0.2, turn_w, w, "turn")
            at(step + LEAD - 1 + 0.3, line_w, w)
            at(step + LEAD - 0.1, quantize_w, w)

        for i in range(4, 8):
            at(i - 2 + 0.2, turn_h, i)
            at(i - 2 + 0.3, line_h, i)
        at(7.5, quantize_h, 1)
        at(16, order_vectors)

        for q in range(QUADS):
            first = BLOCKS * (q + 1)
            at(first - 0.2, open_sums, q)
            for u in range(TILES):
                step = first + 2 * u
                at(step - 0.1, to_rows, q, u, 0)
                at(step + 0.9, to_rows, q, u, 1)
                if (q, u) in VECTOR_SUMS:
                    at(step + 1, bn_half, q, u, 0)
                    at(step + 2, bn_half, q, u, 1)
                    at(step + 2.5, bn_join, q, u)
                    at(step + 3, bn_end, q, u)
                else:
                    at(step + 1, sum_half, q, u, 0)
                    at(step + 2, sum_half, q, u, 1)
                    at(step + 2.5, square_half, q, u, 0)
                    at(step + 3, square_half, q, u, 1)
            known = first + BLOCKS + 2
            for stage in (add_squares, take_root, invert, scale_ratio):
                at(known, stage, q)
            gains = known + 6
            if q >= GROUPS:
                at(max(known, 37), spread_ratio, q)
                for j in range(BLOCKS):
                    at(gains + j, apply_gain, q, j)
            if q >= 2 * GROUPS:
                bg = q % 2
                for stage in (split_coef, turn_coef, copy_coef):
                    at(known + 1, stage, bg)
                for j in range(BLOCKS):
                    at(gains + j - 0.5, join_branch_0, bg, j)
                for c in range(2):
                    for u in range(TILES):
                        step = gains + 4 * c + 4 + u
                        at(step, close, bg, u, c, ("product", "row", "row")[(4 * c + u) % 3])
                        at(step + 12, take_out, bg, u, c, "vector" if bg == 1 and u % 2 == 1 else "scalar")

        for step, place, stage, args in sorted(plan):
            stage(*args)
